import numpy as np
import ml_dtypes


def mxq(x, axis, fmt="e4m3"):
    dtype, down = {"e4m3": (ml_dtypes.float8_e4m3fn, 7), "e5m2": (ml_dtypes.float8_e5m2, 14)}[fmt]
    v = np.moveaxis(np.asarray(x, np.float32).astype(ml_dtypes.bfloat16).astype(np.float64), axis, -1)
    blocks = v.reshape(v.shape[:-1] + (-1, 32))
    amax = np.abs(blocks).max(-1, keepdims=True)
    byte = np.maximum(np.where(amax > 0, np.frexp(amax)[1] - 1 + 127, 0) - down, 1)
    scale = np.exp2(byte - 127.0)
    codes = (blocks / scale).astype(np.float32).astype(dtype).astype(np.float64)
    return np.moveaxis((codes * scale).reshape(v.shape), -1, axis)


WIDE = False


def mx_kscale(k):
    if not WIDE:
        return np.ones(k)
    levels = np.array([10, -10, 5, -5, 0])
    if k % 512:
        return np.exp2(np.random.permutation(np.resize(levels, k // 32))).repeat(32)
    a = np.empty((k // 512, 16))
    for p in range(k // 512):
        a[p, :8] = np.random.permutation(np.resize(levels, 8))
        for g in range(8):
            far = levels[np.abs(levels - a[p, g]) >= 10]
            a[p, g + 8] = far[np.random.randint(len(far))]
    return np.exp2(a.ravel()).repeat(32)


BF16 = ml_dtypes.bfloat16


def bf(x):
    return np.asarray(x, np.float32).astype(BF16)


def f64(x):
    return np.asarray(x).astype(np.float64)


P, N, Z, H1, H2, C = 8, 256, 16, 512, 2048, 256
EPS = 1e-5


def batch_norm(h, gamma, beta):
    mu = h.mean(axis=1, keepdims=True)
    var = h.var(axis=1, keepdims=True)
    return (h - mu) * (1.0 / np.sqrt(var + EPS)) * gamma[:, None, :] + beta[:, None, :]


def setup_inputs():
    r = np.random.standard_normal
    t = mx_kscale(H2)
    sd = np.where(np.random.random((P, 1, H2)) < 0.25, np.sqrt(EPS), 1.0)
    return {"h7_pre": bf((r((P, N, H2)) + 0.5 * r((P, 1, H2))) * sd),
            "g7": bf((1.0 + 0.1 * r((P, H2))) * t),
            "be7": bf(0.3 * r((P, H2)) * t),
            "W8": bf(1.5 * r((P, C, H2)) / np.sqrt(H2) / t),
            "b8": bf(0.5 * r((P, C)))}


def reference(h7_pre, g7, be7, W8, b8):
    a = np.maximum(batch_norm(f64(h7_pre), f64(g7), f64(be7)), 0.0)
    y = (mxq(a, 2, "e4m3") @ mxq(f64(W8), 2, "e4m3").transpose(0, 2, 1)) + f64(b8)[:, None, :]
    em = 1.0 / (1.0 + np.exp(-y))
    return em.transpose(1, 0, 2)

@@ -1,0 +1,285 @@
+from contextlib import ExitStack
+
+import concourse.mybir as mybir
+from concourse.masks import make_identity
+
+F32 = mybir.dt.float32
+BF16 = mybir.dt.bfloat16
+U32 = mybir.dt.uint32
+U8 = mybir.dt.uint8
+FP8X4 = mybir.dt.float8_e4m3fn_x4
+ALU = mybir.AluOpType
+ACT = mybir.ActivationFunctionType
+
+NBLK, ROWS, K, CH = 8, 256, 2048, 256
+EPS = 1e-5
+P = 128
+PASSES = K // 512
+STEPS = NBLK * PASSES
+FLOPS = 2 * NBLK * ROWS * CH * K
+
+UNIT = 2
+N_UNITS = STEPS // UNIT
+LAG_W = 1
+LAG_CHAIN = 3
+LAG_NORM = 5
+LAG_MX = 2
+H_BANKS = 6
+
+
+def regroup_on_scalar(s):
+    return s % 3 == 2 and s < 24
+
+
+def tile_decoder_pb_kernel(tc, h7_pre, g7, be7, W8, b8, out):
+    nc = tc.nc
+    with ExitStack() as ctx:
+        const = ctx.enter_context(tc.tile_pool(name="const", bufs=1))
+        resident = ctx.enter_context(tc.tile_pool(name="resident", bufs=NBLK))
+        small = ctx.enter_context(tc.tile_pool(name="small", bufs=4))
+        work = ctx.enter_context(tc.tile_pool(name="work", bufs=4))
+        codes = ctx.enter_context(tc.tile_pool(name="codes", bufs=3))
+        psum = ctx.enter_context(tc.psum_pool(name="psum", bufs=1))
+
+        hx = []
+        wx = []
+        for p in range(NBLK):
+            hx_p = resident.tile([P, 2 * K], BF16, name="hx_p", tag="hx")
+            wx_p = resident.tile([P, 2 * K], BF16, name="wx_p", tag="wx")
+            hx.append(hx_p)
+            wx.append(wx_p)
+
+        def load(dst, src, k0, k1):
+            nc.sync.dma_start(
+                out=dst[:].rearrange("n (t k) -> n t k", t=2)[:, :, k0:k1],
+                in_=src.rearrange("(t n) k -> n t k", t=2)[:, :, k0:k1],
+            )
+
+        gb_raw = const.tile([P, 512], BF16)
+        nc.vector.memset(gb_raw[64:128, :], 0.0)
+        nc.scalar.dma_start(out=gb_raw[0:32, :], in_=g7.rearrange("p (g k) -> (p g) k", k=512))
+        nc.scalar.dma_start(out=gb_raw[32:64, :], in_=be7.rearrange("p (g k) -> (p g) k", k=512))
+        bb = const.tile([P, NBLK * CH], BF16)
+
+        load(hx[0], h7_pre[0], 0, 512)
+        load(hx[0], h7_pre[0], 512, 1024)
+        load(wx[0], W8[0], 0, 1024)
+        load(hx[0], h7_pre[0], 1024, 2048)
+        load(wx[0], W8[0], 1024, 2048)
+        for p in range(1, NBLK):
+            load(hx[p], h7_pre[p], 0, K)
+            load(wx[p], W8[p], 0, K)
+            if p == 1:
+                nc.sync.dma_start(out=bb[:], in_=b8.rearrange("p c -> (p c)").partition_broadcast(P))
+
+        ident = const.tile([P, P], F32)
+        make_identity(nc, ident[:])
+        neg_half = const.tile([P, 4 * UNIT], F32)
+        nc.gpsimd.memset(neg_half[:], -0.5)
+        warm = const.tile([P, 1], F32)
+        nc.vector.memset(warm[:], 0.0)
+        nc.scalar.activation(out=warm[:], in_=warm[:], func=ACT.Sigmoid)
+
+        gb_t = psum.tile([P, 512], F32, name="gb_t", tag="wt")
+        gb_words = gb_raw[:].bitcast(F32)
+        for u in range(2):
+            nc.tensor.transpose(gb_t[:, u * P : (u + 1) * P], gb_words[:, u:256:2], ident[:])
+        gb = const.tile([P, 256], F32)
+        nc.vector.tensor_copy(
+            out=gb[:].rearrange("q (r u e) -> q u r e", u=2, e=2),
+            in_=gb_t[:, 0:256].bitcast(BF16).rearrange("q (u r e) -> q u r e", u=2, e=2)[:, :, 0:64, :],
+        )
+
+        st = const.tile([P, NBLK * 8 * 6], F32)
+        sc = const.tile([P, NBLK * 16], F32)
+        bi = const.tile([P, NBLK * 16], F32)
+        out_v = out.rearrange("(t n) p c -> n t p c", t=2)
+        live = {}
+
+        def transposes(bank, src, g):
+            words = src[:].bitcast(F32)
+            for u in range(2):
+                for t in range(2):
+                    nc.tensor.transpose(
+                        bank[:, u * 256 + t * P : u * 256 + (t + 1) * P],
+                        words[:, t * 1024 + g * 256 + u : t * 1024 + (g + 1) * 256 : 2],
+                        ident[:],
+                    )
+
+        def unit_stats(j):
+            w = 4 * UNIT
+            return st[:, j * 3 * w : (j + 1) * 3 * w].rearrange("q (c s) -> q c s", s=3)
+
+        def rstd_on_pool(j):
+            w = 4 * UNIT
+            var = small.tile([P, w], F32, name="var", tag="var")
+            nc.gpsimd.tensor_scalar(
+                out=var[:], in0=unit_stats(j)[:, :, 2], scalar1=1.0 / ROWS, scalar2=EPS, op0=ALU.mult, op1=ALU.add
+            )
+            rstd = small.tile([P, w], F32, name="rstd", tag="rstd")
+            live[("rstd", j)] = rstd
+            nc.gpsimd.tensor_tensor(out=rstd[:], in0=var[:], in1=neg_half[:], op=ALU.pow)
+
+        def scale_and_shift(j, part):
+            w = 4 * UNIT
+            cols = slice(j * w, (j + 1) * w)
+            if part == 0:
+                nc.vector.tensor_tensor(out=sc[:, cols], in0=live[("rstd", j)][:], in1=gb[:, cols], op=ALU.mult)
+            elif part == 1:
+                ms = small.tile([P, w], F32, name="ms", tag="ms")
+                live[("ms", j)] = ms
+                nc.vector.tensor_tensor(out=ms[:], in0=unit_stats(j)[:, :, 1], in1=sc[:, cols], op=ALU.mult)
+            else:
+                nc.vector.tensor_tensor(
+                    out=bi[:, cols], in0=gb[:, 128 + j * w : 128 + (j + 1) * w], in1=live[("ms", j)][:], op=ALU.subtract
+                )
+
+        def norm(s):
+            bank = live[("hb", s)][:].bitcast(BF16).rearrange("q (u n e) -> q u n e", u=2, e=2)
+            planes = work.tile([P, 4 * ROWS], BF16, name="planes", tag="planes")
+            live[("planes", s)] = planes
+            for u in range(2):
+                for e in range(2):
+                    col = (2 * s + u) * 2 + e
+                    j = 2 * u + e
+                    nc.scalar.activation(
+                        out=planes[:, j * ROWS : (j + 1) * ROWS],
+                        in_=bank[:, u, :, e],
+                        func=ACT.Relu,
+                        bias=bi[:, col : col + 1],
+                        scale=sc[:, col : col + 1],
+                    )
+
+        def regroup(s):
+            grouped = work.tile([P, 4 * ROWS], BF16, name="grouped", tag="grouped", align_bytes=64)
+            live[("grouped", s)] = grouped
+            dst = grouped[:].rearrange("q (c i j) -> q c j i", i=4, j=4)
+            src = live[("planes", s)][:].rearrange("q (j c i) -> q c j i", i=4, j=4)
+            if regroup_on_scalar(s):
+                nc.scalar.copy(out=dst, in_=src)
+            else:
+                nc.vector.tensor_copy(out=dst, in_=src)
+
+        def quantise(kind, s, width):
+            p, g = s // PASSES, s % PASSES
+            if g == 0:
+                words = codes.tile([P, PASSES * width], U32, name="words", tag=kind + "_words", align_bytes=64)
+                scales = codes.tile([P, PASSES * width], U8, name="scales", tag=kind + "_scales", align_bytes=64)
+                live[(kind, p)] = (words, scales)
+            words, scales = live[(kind, p)]
+            nc.vector.quantize_mx(
+                out=words[:, g * width : (g + 1) * width].bitcast(FP8X4),
+                scales=scales[:, g * width : (g + 1) * width],
+                in_=live[("grouped" if kind == "a" else "wg", s)][:],
+            )
+
+        def mx_pass(acc_cols, p, g, t):
+            a_words, a_scales = live[("a", p)]
+            w_words, w_scales = live[("w", p)]
+            a_cols = slice(g * ROWS + t * P, g * ROWS + (t + 1) * P)
+            w_cols = slice(g * CH, (g + 1) * CH)
+            nc.tensor.matmul_mx(
+                out=acc_cols,
+                lhsT=a_words[:, a_cols].bitcast(FP8X4),
+                lhsT_scale=a_scales[:, a_cols],
+                rhs=w_words[:, w_cols].bitcast(FP8X4),
+                rhs_scale=w_scales[:, w_cols],
+                start=(g == 0),
+                stop=(g == PASSES - 1),
+            )
+
+        def product(p):
+            acc = psum.tile([P, 512], F32, name="acc", tag="acc")
+            live[("acc", p)] = acc
+            for t in range(2):
+                for g in range(PASSES):
+                    mx_pass(acc[:, t * CH : (t + 1) * CH], p, g, t)
+
+        def add_bias(p):
+            y = work.tile([P, 2 * CH], F32, name="y", tag="y")
+            live[("y", p)] = y
+            nc.vector.tensor_tensor(
+                out=y[:].rearrange("n (t c) -> n t c", t=2),
+                in0=live[("acc", p)][:].rearrange("n (t c) -> n t c", t=2),
+                in1=bb[:, p * CH : (p + 1) * CH].unsqueeze(1).to_broadcast([P, 2, CH]),
+                op=ALU.add,
+            )
+
+        def sigmoid_store(p):
+            o = work.tile([P, 2 * CH], F32, name="o", tag="o")
+            nc.scalar.activation(out=o[:], in_=live[("y", p)][:], func=ACT.Sigmoid)
+            nc.sync.dma_start(out=out_v[:, :, p, :], in_=o[:].rearrange("n (t c) -> n t c", t=2))
+
+        last = NBLK - 1
+        mx_at = {}
+        add_at = {}
+        sig_at = {}
+        for tau in range(STEPS + LAG_NORM + 3):
+            s_h, s_w, s_n = tau, tau - LAG_W, tau - LAG_NORM
+            if s_h < STEPS:
+                hb = psum.tile([P, 512], F32, name="hb", tag="hb", bufs=H_BANKS)
+                live[("hb", s_h)] = hb
+                transposes(hb, hx[s_h // PASSES], s_h % PASSES)
+            if 0 <= s_w < STEPS:
+                wt = psum.tile([P, 512], F32, name="wt", tag="wt")
+                live[("wt", s_w)] = wt
+                transposes(wt, wx[s_w // PASSES], s_w % PASSES)
+            if tau in mx_at:
+                product(mx_at[tau])
+            if tau in add_at:
+                add_bias(add_at[tau])
+            j_c = tau - LAG_CHAIN - (UNIT - 1)
+            chain_now = j_c >= 0 and j_c % UNIT == 0 and j_c // UNIT < N_UNITS
+            j_c = j_c // UNIT
+            if chain_now:
+                scale_and_shift(j_c, 0)
+            if s_h < STEPS:
+                hab = live[("hb", s_h)][:].bitcast(BF16)
+                nc.vector.bn_stats(out=st[:, 2 * s_h * 6 : (2 * s_h + 1) * 6], in_=hab[:, 0:512])
+            if chain_now:
+                scale_and_shift(j_c, 1)
+            if s_h < STEPS:
+                nc.vector.bn_stats(out=st[:, (2 * s_h + 1) * 6 : (2 * s_h + 2) * 6], in_=hab[:, 512:1024])
+                if s_h % UNIT == UNIT - 1:
+                    rstd_on_pool(s_h // UNIT)
+            if chain_now:
+                scale_and_shift(j_c, 2)
+            if tau in sig_at:
+                sigmoid_store(sig_at[tau])
+            if 0 <= s_n < STEPS:
+                norm(s_n)
+            if 0 <= s_w < STEPS:
+                wg = work.tile([P, 4 * CH], BF16, name="wg", tag="wg", align_bytes=64)
+                live[("wg", s_w)] = wg
+                nc.scalar.copy(
+                    out=wg[:].bitcast(F32).rearrange("q (c u) -> q c u", u=2),
+                    in_=live[("wt", s_w)][:].rearrange("q (u c) -> q c u", u=2),
+                )
+            if 0 <= s_w - 1 < STEPS:
+                quantise("w", s_w - 1, CH)
+            s_q = s_n - 2
+            if 0 <= s_q < STEPS:
+                quantise("a", s_q, ROWS)
+            if 0 <= s_n - 1 < STEPS:
+                regroup(s_n - 1)
+            if 0 <= s_q < STEPS:
+                p, g = s_q // PASSES, s_q % PASSES
+                if p == last:
+                    if g == 0:
+                        for t in range(2):
+                            acc_t = psum.tile([P, 512], F32, name="acc_t", tag="hb", bufs=H_BANKS)
+                            live[("acc_t", t)] = acc_t
+                    for t in range(2):
+                        mx_pass(live[("acc_t", t)][:, 0:CH], p, g, t)
+                elif g == PASSES - 1:
+                    mx_at[tau + LAG_MX] = p
+                    add_at[tau + LAG_MX + 1] = p
+                    sig_at[tau + LAG_MX + 2] = p
+        for t in range(2):
+            y_t = work.tile([P, CH], F32, name="y_t", tag="y_t", bufs=2)
+            nc.vector.tensor_tensor(
+                out=y_t[:], in0=live[("acc_t", t)][:, 0:CH], in1=bb[:, last * CH : (last + 1) * CH], op=ALU.add
+            )
+            o_t = work.tile([P, CH], F32, name="o_t", tag="o_t", bufs=2)
+            nc.scalar.activation(out=o_t[:], in_=y_t[:], func=ACT.Sigmoid)
+            nc.sync.dma_start(out=out_v[:, t, last, :], in_=o_t[:])

@@ -21,14 +21,14 @@ FLOPS = 2 * NBLK * ROWS * CH * K
 UNIT = 2
 N_UNITS = STEPS // UNIT
 LAG_W = 1
-LAG_CHAIN = 3
-LAG_NORM = 5
+LAG_CHAIN = 2
+LAG_NORM = 4
 LAG_MX = 2
 H_BANKS = 6
 
 
 def regroup_on_scalar(s):
-    return s % 3 == 2 and s < 24
+    return s % 2 == 1 and s < 24
 
 
 def tile_decoder_pb_kernel(tc, h7_pre, g7, be7, W8, b8, out):
@@ -40,6 +40,7 @@ def tile_decoder_pb_kernel(tc, h7_pre, g7, be7, W8, b8, out):
         work = ctx.enter_context(tc.tile_pool(name="work", bufs=4))
         codes = ctx.enter_context(tc.tile_pool(name="codes", bufs=3))
         psum = ctx.enter_context(tc.psum_pool(name="psum", bufs=1))
+        ctx.enter_context(tc.manual_schedule())
 
         hx = []
         wx = []
@@ -74,11 +75,9 @@ def tile_decoder_pb_kernel(tc, h7_pre, g7, be7, W8, b8, out):
 
         ident = const.tile([P, P], F32)
         make_identity(nc, ident[:])
-        neg_half = const.tile([P, 4 * UNIT], F32)
-        nc.gpsimd.memset(neg_half[:], -0.5)
         warm = const.tile([P, 1], F32)
-        nc.vector.memset(warm[:], 0.0)
-        nc.scalar.activation(out=warm[:], in_=warm[:], func=ACT.Sigmoid)
+        nc.vector.memset(warm[:], 1.0)
+        nc.scalar.activation(out=warm[:], in_=warm[:], func=ACT.Abs_reciprocal_sqrt)
 
         gb_t = psum.tile([P, 512], F32, name="gb_t", tag="wt")
         gb_words = gb_raw[:].bitcast(F32)
@@ -110,15 +109,12 @@ def tile_decoder_pb_kernel(tc, h7_pre, g7, be7, W8, b8, out):
             w = 4 * UNIT
             return st[:, j * 3 * w : (j + 1) * 3 * w].rearrange("q (c s) -> q c s", s=3)
 
-        def rstd_on_pool(j):
-            w = 4 * UNIT
-            var = small.tile([P, w], F32, name="var", tag="var")
-            nc.gpsimd.tensor_scalar(
-                out=var[:], in0=unit_stats(j)[:, :, 2], scalar1=1.0 / ROWS, scalar2=EPS, op0=ALU.mult, op1=ALU.add
-            )
-            rstd = small.tile([P, w], F32, name="rstd", tag="rstd")
+        def rstd_on_scalar(j):
+            rstd = small.tile([P, 4 * UNIT], F32, name="rstd", tag="rstd")
             live[("rstd", j)] = rstd
-            nc.gpsimd.tensor_tensor(out=rstd[:], in0=var[:], in1=neg_half[:], op=ALU.pow)
+            nc.scalar.activation(
+                out=rstd[:], in_=unit_stats(j)[:, :, 2], func=ACT.Abs_reciprocal_sqrt, scale=1.0 / ROWS, bias=EPS
+            )
 
         def scale_and_shift(j, part):
             w = 4 * UNIT
@@ -196,7 +192,7 @@ def tile_decoder_pb_kernel(tc, h7_pre, g7, be7, W8, b8, out):
                     mx_pass(acc[:, t * CH : (t + 1) * CH], p, g, t)
 
         def add_bias(p):
-            y = work.tile([P, 2 * CH], F32, name="y", tag="y")
+            y = work.tile([P, 2 * CH], F32, name="y", tag="y", bufs=NBLK)
             live[("y", p)] = y
             nc.vector.tensor_tensor(
                 out=y[:].rearrange("n (t c) -> n t c", t=2),
@@ -214,6 +210,7 @@ def tile_decoder_pb_kernel(tc, h7_pre, g7, be7, W8, b8, out):
         mx_at = {}
         add_at = {}
         sig_at = {}
+        sig_ready = []
         for tau in range(STEPS + LAG_NORM + 3):
             s_h, s_w, s_n = tau, tau - LAG_W, tau - LAG_NORM
             if s_h < STEPS:
@@ -240,14 +237,18 @@ def tile_decoder_pb_kernel(tc, h7_pre, g7, be7, W8, b8, out):
                 scale_and_shift(j_c, 1)
             if s_h < STEPS:
                 nc.vector.bn_stats(out=st[:, (2 * s_h + 1) * 6 : (2 * s_h + 2) * 6], in_=hab[:, 512:1024])
-                if s_h % UNIT == UNIT - 1:
-                    rstd_on_pool(s_h // UNIT)
             if chain_now:
                 scale_and_shift(j_c, 2)
-            if tau in sig_at:
-                sigmoid_store(sig_at[tau])
+            if 0 < s_h <= STEPS and s_h % UNIT == 0:
+                rstd_on_scalar(s_h // UNIT - 1)
             if 0 <= s_n < STEPS:
                 norm(s_n)
+            if tau > STEPS:
+                for p in sig_ready[:2]:
+                    sigmoid_store(p)
+                sig_ready = sig_ready[2:]
+            if tau in sig_at:
+                sig_ready.append(sig_at[tau])
             if 0 <= s_w < STEPS:
                 wg = work.tile([P, 4 * CH], BF16, name="wg", tag="wg", align_bytes=64)
                 live[("wg", s_w)] = wg
@@ -274,7 +275,9 @@ def tile_decoder_pb_kernel(tc, h7_pre, g7, be7, W8, b8, out):
                 elif g == PASSES - 1:
                     mx_at[tau + LAG_MX] = p
                     add_at[tau + LAG_MX + 1] = p
-                    sig_at[tau + LAG_MX + 2] = p
+                    sig_at[tau + LAG_MX + 1] = p
+        for p in sig_ready:
+            sigmoid_store(p)
         for t in range(2):
             y_t = work.tile([P, CH], F32, name="y_t", tag="y_t", bufs=2)
             nc.vector.tensor_tensor(

@@ -19,16 +19,13 @@ STEPS = NBLK * PASSES
 FLOPS = 2 * NBLK * ROWS * CH * K
 
 UNIT = 2
-N_UNITS = STEPS // UNIT
+PAIRS = STEPS // UNIT
 LAG_W = 1
-LAG_CHAIN = 2
-LAG_NORM = 4
-LAG_MX = 2
 H_BANKS = 6
 
 
-def regroup_on_scalar(s):
-    return s % 2 == 1 and s < 24
+def regroup_on_gpsimd(s):
+    return s % 2 == 0 and s < STEPS - 2 * UNIT
 
 
 def tile_decoder_pb_kernel(tc, h7_pre, g7, be7, W8, b8, out):
@@ -116,25 +113,24 @@ def tile_decoder_pb_kernel(tc, h7_pre, g7, be7, W8, b8, out):
                 out=rstd[:], in_=unit_stats(j)[:, :, 2], func=ACT.Abs_reciprocal_sqrt, scale=1.0 / ROWS, bias=EPS
             )
 
-        def scale_and_shift(j, part):
+        def scale_and_shift(j):
             w = 4 * UNIT
             cols = slice(j * w, (j + 1) * w)
-            if part == 0:
-                nc.vector.tensor_tensor(out=sc[:, cols], in0=live[("rstd", j)][:], in1=gb[:, cols], op=ALU.mult)
-            elif part == 1:
-                ms = small.tile([P, w], F32, name="ms", tag="ms")
-                live[("ms", j)] = ms
-                nc.vector.tensor_tensor(out=ms[:], in0=unit_stats(j)[:, :, 1], in1=sc[:, cols], op=ALU.mult)
-            else:
-                nc.vector.tensor_tensor(
-                    out=bi[:, cols], in0=gb[:, 128 + j * w : 128 + (j + 1) * w], in1=live[("ms", j)][:], op=ALU.subtract
-                )
+            ms = small.tile([P, w], F32, name="ms", tag="ms")
+            eng = nc.gpsimd
+            eng.tensor_tensor(out=sc[:, cols], in0=live[("rstd", j)][:], in1=gb[:, cols], op=ALU.mult)
+            eng.tensor_tensor(out=ms[:], in0=unit_stats(j)[:, :, 1], in1=sc[:, cols], op=ALU.mult)
+            eng.tensor_tensor(
+                out=bi[:, cols], in0=gb[:, 128 + j * w : 128 + (j + 1) * w], in1=ms[:], op=ALU.subtract
+            )
 
-        def norm(s):
+        def norm(s, halves):
             bank = live[("hb", s)][:].bitcast(BF16).rearrange("q (u n e) -> q u n e", u=2, e=2)
-            planes = work.tile([P, 4 * ROWS], BF16, name="planes", tag="planes")
-            live[("planes", s)] = planes
-            for u in range(2):
+            if 0 in halves:
+                planes = work.tile([P, 4 * ROWS], BF16, name="planes", tag="planes", bufs=6)
+                live[("planes", s)] = planes
+            planes = live[("planes", s)]
+            for u in halves:
                 for e in range(2):
                     col = (2 * s + u) * 2 + e
                     j = 2 * u + e
@@ -147,18 +143,24 @@ def tile_decoder_pb_kernel(tc, h7_pre, g7, be7, W8, b8, out):
                     )
 
         def regroup(s):
-            grouped = work.tile([P, 4 * ROWS], BF16, name="grouped", tag="grouped", align_bytes=64)
+            on_gpsimd = regroup_on_gpsimd(s)
+            if on_gpsimd:
+                grouped = work.tile([P, 4 * ROWS], BF16, name="grouped_g", tag="grouped_g", align_bytes=64, bufs=1)
+            else:
+                grouped = work.tile([P, 4 * ROWS], BF16, name="grouped", tag="grouped", align_bytes=64)
             live[("grouped", s)] = grouped
             dst = grouped[:].rearrange("q (c i j) -> q c j i", i=4, j=4)
             src = live[("planes", s)][:].rearrange("q (j c i) -> q c j i", i=4, j=4)
-            if regroup_on_scalar(s):
-                nc.scalar.copy(out=dst, in_=src)
+            if on_gpsimd:
+                nc.gpsimd.tensor_scalar(
+                    out=dst, in0=src, scalar1=1.0, scalar2=0.0, op0=ALU.mult, op1=ALU.add
+                )
             else:
                 nc.vector.tensor_copy(out=dst, in_=src)
 
         def quantise(kind, s, width):
             p, g = s // PASSES, s % PASSES
-            if g == 0:
+            if (kind, p) not in live:
                 words = codes.tile([P, PASSES * width], U32, name="words", tag=kind + "_words", align_bytes=64)
                 scales = codes.tile([P, PASSES * width], U8, name="scales", tag=kind + "_scales", align_bytes=64)
                 live[(kind, p)] = (words, scales)
@@ -207,75 +209,99 @@ def tile_decoder_pb_kernel(tc, h7_pre, g7, be7, W8, b8, out):
             nc.sync.dma_start(out=out_v[:, :, p, :], in_=o[:].rearrange("n (t c) -> n t c", t=2))
 
         last = NBLK - 1
-        mx_at = {}
-        add_at = {}
-        sig_at = {}
+
+        def h_transposes(s):
+            hb = psum.tile([P, 512], F32, name="hb", tag="hb", bufs=H_BANKS)
+            live[("hb", s)] = hb
+            transposes(hb, hx[s // PASSES], s % PASSES)
+
+        def w_transposes(s):
+            wt = psum.tile([P, 512], F32, name="wt", tag="wt")
+            live[("wt", s)] = wt
+            transposes(wt, wx[s // PASSES], s % PASSES)
+
+        def w_copy(s):
+            wg = work.tile([P, 4 * CH], BF16, name="wg", tag="wg", align_bytes=64)
+            live[("wg", s)] = wg
+            nc.scalar.copy(
+                out=wg[:].bitcast(F32).rearrange("q (c u) -> q c u", u=2),
+                in_=live[("wt", s)][:].rearrange("q (u c) -> q c u", u=2),
+            )
+
+        def statistics(s):
+            hab = live[("hb", s)][:].bitcast(BF16)
+            for u in range(2):
+                c = 2 * s + u
+                nc.vector.bn_stats(out=st[:, c * 6 : (c + 1) * 6], in_=hab[:, u * 512 : (u + 1) * 512])
+
+        def last_passes(s):
+            if s % PASSES == 0:
+                for t in range(2):
+                    acc_t = psum.tile([P, 512], F32, name="acc_t", tag="hb", bufs=H_BANKS)
+                    live[("acc_t", t)] = acc_t
+            for t in range(2):
+                mx_pass(live[("acc_t", t)][:, 0:CH], last, s % PASSES, t)
+
+        def passes_of(j):
+            return range(UNIT * j, UNIT * j + UNIT) if 0 <= j < PAIRS else range(0)
+
         sig_ready = []
-        for tau in range(STEPS + LAG_NORM + 3):
-            s_h, s_w, s_n = tau, tau - LAG_W, tau - LAG_NORM
-            if s_h < STEPS:
-                hb = psum.tile([P, 512], F32, name="hb", tag="hb", bufs=H_BANKS)
-                live[("hb", s_h)] = hb
-                transposes(hb, hx[s_h // PASSES], s_h % PASSES)
-            if 0 <= s_w < STEPS:
-                wt = psum.tile([P, 512], F32, name="wt", tag="wt")
-                live[("wt", s_w)] = wt
-                transposes(wt, wx[s_w // PASSES], s_w % PASSES)
-            if tau in mx_at:
-                product(mx_at[tau])
-            if tau in add_at:
-                add_bias(add_at[tau])
-            j_c = tau - LAG_CHAIN - (UNIT - 1)
-            chain_now = j_c >= 0 and j_c % UNIT == 0 and j_c // UNIT < N_UNITS
-            j_c = j_c // UNIT
-            if chain_now:
-                scale_and_shift(j_c, 0)
-            if s_h < STEPS:
-                hab = live[("hb", s_h)][:].bitcast(BF16)
-                nc.vector.bn_stats(out=st[:, 2 * s_h * 6 : (2 * s_h + 1) * 6], in_=hab[:, 0:512])
-            if chain_now:
-                scale_and_shift(j_c, 1)
-            if s_h < STEPS:
-                nc.vector.bn_stats(out=st[:, (2 * s_h + 1) * 6 : (2 * s_h + 2) * 6], in_=hab[:, 512:1024])
-            if chain_now:
-                scale_and_shift(j_c, 2)
-            if 0 < s_h <= STEPS and s_h % UNIT == 0:
-                rstd_on_scalar(s_h // UNIT - 1)
-            if 0 <= s_n < STEPS:
-                norm(s_n)
-            if tau > STEPS:
-                for p in sig_ready[:2]:
+        for s in passes_of(0):
+            h_transposes(s)
+        for tau in range(PAIRS + 3):
+            w_now, h_next = passes_of(tau - LAG_W), passes_of(tau + 1)
+            for i in range(UNIT):
+                if w_now:
+                    w_transposes(w_now[i])
+                if h_next:
+                    h_transposes(h_next[i])
+            p_mx = (tau - 4) // 2 if tau % 2 == 0 and 4 <= tau else -1
+            if 0 <= p_mx < last:
+                product(p_mx)
+            for s in passes_of(tau - 2):
+                if regroup_on_gpsimd(s):
+                    regroup(s)
+            for s in passes_of(tau):
+                statistics(s)
+            p_add = (tau - 5) // 2 if tau % 2 == 1 and 5 <= tau else -1
+            if 0 <= p_add < last:
+                add_bias(p_add)
+            n_now = passes_of(tau - 1)
+            if n_now:
+                norm(n_now[0], (0, 1))
+            if w_now:
+                w_copy(w_now[0])
+            if n_now:
+                norm(n_now[1], (0,))
+            if tau < PAIRS:
+                rstd_on_scalar(tau)
+                scale_and_shift(tau)
+            if n_now:
+                norm(n_now[1], (1,))
+            if w_now:
+                w_copy(w_now[1])
+            if tau >= PAIRS:
+                for p in sig_ready[:3]:
                     sigmoid_store(p)
-                sig_ready = sig_ready[2:]
-            if tau in sig_at:
-                sig_ready.append(sig_at[tau])
-            if 0 <= s_w < STEPS:
-                wg = work.tile([P, 4 * CH], BF16, name="wg", tag="wg", align_bytes=64)
-                live[("wg", s_w)] = wg
-                nc.scalar.copy(
-                    out=wg[:].bitcast(F32).rearrange("q (c u) -> q c u", u=2),
-                    in_=live[("wt", s_w)][:].rearrange("q (u c) -> q c u", u=2),
-                )
-            if 0 <= s_w - 1 < STEPS:
-                quantise("w", s_w - 1, CH)
-            s_q = s_n - 2
-            if 0 <= s_q < STEPS:
-                quantise("a", s_q, ROWS)
-            if 0 <= s_n - 1 < STEPS:
-                regroup(s_n - 1)
-            if 0 <= s_q < STEPS:
-                p, g = s_q // PASSES, s_q % PASSES
-                if p == last:
-                    if g == 0:
-                        for t in range(2):
-                            acc_t = psum.tile([P, 512], F32, name="acc_t", tag="hb", bufs=H_BANKS)
-                            live[("acc_t", t)] = acc_t
-                    for t in range(2):
-                        mx_pass(live[("acc_t", t)][:, 0:CH], p, g, t)
-                elif g == PASSES - 1:
-                    mx_at[tau + LAG_MX] = p
-                    add_at[tau + LAG_MX + 1] = p
-                    sig_at[tau + LAG_MX + 1] = p
+                sig_ready = sig_ready[3:]
+            if 0 <= p_add < last:
+                sig_ready.append(p_add)
+            own = [s for s in passes_of(tau - 2) if not regroup_on_gpsimd(s)]
+            other = [s for s in passes_of(tau - 2) if regroup_on_gpsimd(s)]
+            w_q = passes_of(tau - LAG_W - 1)
+            for s in own:
+                regroup(s)
+            if w_q:
+                quantise("w", w_q[0], CH)
+            for s in own:
+                quantise("a", s, ROWS)
+            if w_q:
+                quantise("w", w_q[1], CH)
+            for s in other:
+                quantise("a", s, ROWS)
+            for s in passes_of(tau - 2):
+                if s // PASSES == last:
+                    last_passes(s)
         for p in sig_ready:
             sigmoid_store(p)
         for t in range(2):

@@ -14,59 +14,68 @@ ACT = mybir.ActivationFunctionType
 NBLK, ROWS, K, CH = 8, 256, 2048, 256
 EPS = 1e-5
 P = 128
-PASSES = K // 512
+KP = 512
+PASSES = K // KP
 STEPS = NBLK * PASSES
 FLOPS = 2 * NBLK * ROWS * CH * K
 
 UNIT = 2
 PAIRS = STEPS // UNIT
-LAG_W = 1
+W_COLS = 4 * UNIT
+V_BLOCKS = ROWS // 4 - 12
+LAG_W = 0
 H_BANKS = 6
 
 
-def regroup_on_gpsimd(s):
-    return s % 2 == 0 and s < STEPS - 2 * UNIT
+def regroup_engine(s):
+    if s % 2 == 1 and s < STEPS - UNIT:
+        return "gpsimd"
+    if 4 <= s < 28:
+        return "shared"
+    return "vector"
+
+
+def norm_on_vector(s):
+    return s == STEPS - 1
 
 
 def tile_decoder_pb_kernel(tc, h7_pre, g7, be7, W8, b8, out):
     nc = tc.nc
     with ExitStack() as ctx:
         const = ctx.enter_context(tc.tile_pool(name="const", bufs=1))
-        resident = ctx.enter_context(tc.tile_pool(name="resident", bufs=NBLK))
+        resident = ctx.enter_context(tc.tile_pool(name="resident", bufs=1))
         small = ctx.enter_context(tc.tile_pool(name="small", bufs=4))
         work = ctx.enter_context(tc.tile_pool(name="work", bufs=4))
         codes = ctx.enter_context(tc.tile_pool(name="codes", bufs=3))
         psum = ctx.enter_context(tc.psum_pool(name="psum", bufs=1))
         ctx.enter_context(tc.manual_schedule())
 
-        hx = []
-        wx = []
-        for p in range(NBLK):
-            hx_p = resident.tile([P, 2 * K], BF16, name="hx_p", tag="hx")
-            wx_p = resident.tile([P, 2 * K], BF16, name="wx_p", tag="wx")
-            hx.append(hx_p)
-            wx.append(wx_p)
+        where = {}
 
-        def load(dst, src, k0, k1):
+        def load(kind, src, p, g0, g1):
+            width = (g1 - g0) * KP
+            raw = resident.tile([P, 2 * width], BF16, name="raw", tag=kind + str(p) + "_" + str(g0))
             nc.sync.dma_start(
-                out=dst[:].rearrange("n (t k) -> n t k", t=2)[:, :, k0:k1],
-                in_=src.rearrange("(t n) k -> n t k", t=2)[:, :, k0:k1],
+                out=raw[:].rearrange("n (t k) -> n t k", t=2),
+                in_=src[p].rearrange("(t n) k -> n t k", t=2)[:, :, g0 * KP : g1 * KP],
             )
+            for g in range(g0, g1):
+                where[(kind, p * PASSES + g)] = (raw, (g - g0) * KP, width)
 
-        gb_raw = const.tile([P, 512], BF16)
+        gb_raw = const.tile([P, KP], BF16)
         nc.vector.memset(gb_raw[64:128, :], 0.0)
-        nc.scalar.dma_start(out=gb_raw[0:32, :], in_=g7.rearrange("p (g k) -> (p g) k", k=512))
-        nc.scalar.dma_start(out=gb_raw[32:64, :], in_=be7.rearrange("p (g k) -> (p g) k", k=512))
         bb = const.tile([P, NBLK * CH], BF16)
 
-        load(hx[0], h7_pre[0], 0, 512)
-        load(hx[0], h7_pre[0], 512, 1024)
-        load(wx[0], W8[0], 0, 1024)
-        load(hx[0], h7_pre[0], 1024, 2048)
-        load(wx[0], W8[0], 1024, 2048)
+        load("h", h7_pre, 0, 0, 1)
+        nc.scalar.dma_start(out=gb_raw[0:32, :], in_=g7.rearrange("p (g k) -> (p g) k", k=KP))
+        nc.scalar.dma_start(out=gb_raw[32:64, :], in_=be7.rearrange("p (g k) -> (p g) k", k=KP))
+        load("h", h7_pre, 0, 1, 2)
+        load("w", W8, 0, 0, 2)
+        load("h", h7_pre, 0, 2, 4)
+        load("w", W8, 0, 2, 4)
         for p in range(1, NBLK):
-            load(hx[p], h7_pre[p], 0, K)
-            load(wx[p], W8[p], 0, K)
+            load("h", h7_pre, p, 0, PASSES)
+            load("w", W8, p, 0, PASSES)
             if p == 1:
                 nc.sync.dma_start(out=bb[:], in_=b8.rearrange("p c -> (p c)").partition_broadcast(P))
 
@@ -76,87 +85,145 @@ def tile_decoder_pb_kernel(tc, h7_pre, g7, be7, W8, b8, out):
         nc.vector.memset(warm[:], 1.0)
         nc.scalar.activation(out=warm[:], in_=warm[:], func=ACT.Abs_reciprocal_sqrt)
 
-        gb_t = psum.tile([P, 512], F32, name="gb_t", tag="wt")
-        gb_words = gb_raw[:].bitcast(F32)
-        for u in range(2):
-            nc.tensor.transpose(gb_t[:, u * P : (u + 1) * P], gb_words[:, u:256:2], ident[:])
-        gb = const.tile([P, 256], F32)
-        nc.vector.tensor_copy(
-            out=gb[:].rearrange("q (r u e) -> q u r e", u=2, e=2),
-            in_=gb_t[:, 0:256].bitcast(BF16).rearrange("q (u r e) -> q u r e", u=2, e=2)[:, :, 0:64, :],
-        )
-
-        st = const.tile([P, NBLK * 8 * 6], F32)
-        sc = const.tile([P, NBLK * 16], F32)
+        st = const.tile([P, NBLK * 16 * 3], F32)
+        gain = const.tile([P, NBLK * 32], F32)
+        shift = const.tile([P, NBLK * 16], F32)
+        sc = const.tile([P, NBLK * 32], F32)
         bi = const.tile([P, NBLK * 16], F32)
         out_v = out.rearrange("(t n) p c -> n t p c", t=2)
         live = {}
 
-        def transposes(bank, src, g):
-            words = src[:].bitcast(F32)
+        def gains_and_shifts():
+            gb_t = psum.tile([P, 512], F32, name="gb_t", tag="wt")
+            gb_words = gb_raw[:].bitcast(F32)
+            for u in range(2):
+                nc.tensor.transpose(gb_t[:, u * P : (u + 1) * P], gb_words[:, u : KP // 2 : 2], ident[:])
+            gb_rows = gb_t[:, 0 : 2 * P].bitcast(BF16).rearrange("q (u r e) -> q u r e", u=2, e=2)
+            rows = NBLK * PASSES
+            for i in range(UNIT):
+                nc.vector.tensor_copy(
+                    out=gain[:].rearrange("q (j m i u e) -> q m i u j e", m=2, i=2, u=2, e=2)[:, 0, i],
+                    in_=gb_rows[:, :, i:rows:UNIT, :],
+                )
+            nc.vector.tensor_copy(
+                out=shift[:].rearrange("q (r u e) -> q u r e", u=2, e=2), in_=gb_rows[:, :, rows : 2 * rows, :]
+            )
+
+        def transposes(bank, kind, s):
+            raw, first, width = where[(kind, s)]
+            words = raw[:].bitcast(F32)
             for u in range(2):
                 for t in range(2):
+                    w0 = (t * width + first) // 2 + u
                     nc.tensor.transpose(
-                        bank[:, u * 256 + t * P : u * 256 + (t + 1) * P],
-                        words[:, t * 1024 + g * 256 + u : t * 1024 + (g + 1) * 256 : 2],
-                        ident[:],
+                        bank[:, u * 256 + t * P : u * 256 + (t + 1) * P], words[:, w0 : w0 - u + 256 : 2], ident[:]
                     )
 
+        def h_transposes(s):
+            hb = psum.tile([P, 512], F32, name="hb", tag="hb", bufs=H_BANKS)
+            live[("hb", s)] = hb
+            transposes(hb, "h", s)
+
+        def w_transposes(s):
+            wt = psum.tile([P, 512], F32, name="wt", tag="wt")
+            live[("wt", s)] = wt
+            transposes(wt, "w", s)
+
         def unit_stats(j):
-            w = 4 * UNIT
-            return st[:, j * 3 * w : (j + 1) * 3 * w].rearrange("q (c s) -> q c s", s=3)
+            return st[:, j * 3 * W_COLS : (j + 1) * 3 * W_COLS].rearrange("q (c s) -> q c s", s=3)
 
-        def rstd_on_scalar(j):
-            rstd = small.tile([P, 4 * UNIT], F32, name="rstd", tag="rstd")
-            live[("rstd", j)] = rstd
+        def statistics(s):
+            hab = live[("hb", s)][:].bitcast(BF16)
+            for u in range(2):
+                c = 2 * s + u
+                nc.vector.bn_stats(out=st[:, c * 6 : (c + 1) * 6], in_=hab[:, u * 512 : (u + 1) * 512])
+
+        def rstd(j):
+            r = small.tile([P, W_COLS], F32, name="r", tag="r")
+            live[("rstd", j)] = r
             nc.scalar.activation(
-                out=rstd[:], in_=unit_stats(j)[:, :, 2], func=ACT.Abs_reciprocal_sqrt, scale=1.0 / ROWS, bias=EPS
+                out=r[:], in_=unit_stats(j)[:, :, 2], func=ACT.Abs_reciprocal_sqrt, scale=1.0 / ROWS, bias=EPS
             )
 
-        def scale_and_shift(j):
-            w = 4 * UNIT
-            cols = slice(j * w, (j + 1) * w)
-            ms = small.tile([P, w], F32, name="ms", tag="ms")
-            eng = nc.gpsimd
-            eng.tensor_tensor(out=sc[:, cols], in0=live[("rstd", j)][:], in1=gb[:, cols], op=ALU.mult)
-            eng.tensor_tensor(out=ms[:], in0=unit_stats(j)[:, :, 1], in1=sc[:, cols], op=ALU.mult)
-            eng.tensor_tensor(
-                out=bi[:, cols], in0=gb[:, 128 + j * w : 128 + (j + 1) * w], in1=ms[:], op=ALU.subtract
-            )
+        def scale_and_shift(j, part):
+            w = W_COLS
+            gains, both = gain[:, 2 * j * w : (2 * j + 1) * w], slice(2 * j * w, (2 * j + 2) * w)
+            if part == 0:
+                nc.vector.tensor_tensor(
+                    out=gain[:, (2 * j + 1) * w : (2 * j + 2) * w], in0=unit_stats(j)[:, :, 1], in1=gains, op=ALU.mult
+                )
+            elif part == 1:
+                nc.vector.tensor_tensor(
+                    out=sc[:, both].rearrange("q (m c) -> q m c", m=2),
+                    in0=gain[:, both].rearrange("q (m c) -> q m c", m=2),
+                    in1=live[("rstd", j)][:].unsqueeze(1).to_broadcast([P, 2, w]),
+                    op=ALU.mult,
+                )
+            else:
+                nc.vector.tensor_tensor(
+                    out=bi[:, j * w : (j + 1) * w],
+                    in0=shift[:, j * w : (j + 1) * w],
+                    in1=sc[:, (2 * j + 1) * w : (2 * j + 2) * w],
+                    op=ALU.subtract,
+                )
 
-        def norm(s, halves):
+        def norm(s, u):
             bank = live[("hb", s)][:].bitcast(BF16).rearrange("q (u n e) -> q u n e", u=2, e=2)
-            if 0 in halves:
+            if u == 0:
                 planes = work.tile([P, 4 * ROWS], BF16, name="planes", tag="planes", bufs=6)
                 live[("planes", s)] = planes
             planes = live[("planes", s)]
-            for u in halves:
-                for e in range(2):
-                    col = (2 * s + u) * 2 + e
-                    j = 2 * u + e
-                    nc.scalar.activation(
-                        out=planes[:, j * ROWS : (j + 1) * ROWS],
-                        in_=bank[:, u, :, e],
-                        func=ACT.Relu,
-                        bias=bi[:, col : col + 1],
-                        scale=sc[:, col : col + 1],
+            for e in range(2):
+                c = s % UNIT * 4 + u * 2 + e
+                sc_col = s // UNIT * 2 * W_COLS + c
+                bi_col = s // UNIT * W_COLS + c
+                j = 2 * u + e
+                dst = planes[:, j * ROWS : (j + 1) * ROWS]
+                scale, bias = sc[:, sc_col : sc_col + 1], bi[:, bi_col : bi_col + 1]
+                if norm_on_vector(s):
+                    nc.vector.tensor_scalar(
+                        out=dst, in0=bank[:, u, :, e], scalar1=scale, scalar2=bias, op0=ALU.mult, op1=ALU.add
                     )
+                else:
+                    nc.scalar.activation(out=dst, in_=bank[:, u, :, e], func=ACT.Relu, bias=bias, scale=scale)
+
+        def regroup_part(s, on_scalar):
+            if ("grouped", s) not in live:
+                grouped = work.tile([P, 4 * ROWS], BF16, name="grouped", tag="grouped", align_bytes=64)
+                live[("grouped", s)] = grouped
+            cols = slice(V_BLOCKS, ROWS // 4) if on_scalar else slice(0, V_BLOCKS)
+            dst = live[("grouped", s)][:].rearrange("q (c i j) -> q c j i", i=4, j=4)[:, cols]
+            src = live[("planes", s)][:].rearrange("q (j c i) -> q c j i", i=4, j=4)[:, cols]
+            if on_scalar:
+                nc.scalar.copy(out=dst, in_=src)
+            else:
+                nc.vector.tensor_copy(out=dst, in_=src)
 
         def regroup(s):
-            on_gpsimd = regroup_on_gpsimd(s)
-            if on_gpsimd:
+            engine = regroup_engine(s)
+            if engine == "gpsimd":
                 grouped = work.tile([P, 4 * ROWS], BF16, name="grouped_g", tag="grouped_g", align_bytes=64, bufs=1)
             else:
                 grouped = work.tile([P, 4 * ROWS], BF16, name="grouped", tag="grouped", align_bytes=64)
             live[("grouped", s)] = grouped
             dst = grouped[:].rearrange("q (c i j) -> q c j i", i=4, j=4)
             src = live[("planes", s)][:].rearrange("q (j c i) -> q c j i", i=4, j=4)
-            if on_gpsimd:
-                nc.gpsimd.tensor_scalar(
-                    out=dst, in0=src, scalar1=1.0, scalar2=0.0, op0=ALU.mult, op1=ALU.add
-                )
+            if engine == "gpsimd":
+                nc.gpsimd.tensor_scalar(out=dst, in0=src, scalar1=1.0, scalar2=0.0, op0=ALU.mult, op1=ALU.add)
+            elif engine == "scalar":
+                nc.scalar.copy(out=dst, in_=src)
+            elif norm_on_vector(s):
+                nc.vector.tensor_scalar(out=dst, in0=src, scalar1=0.0, scalar2=None, op0=ALU.max)
             else:
                 nc.vector.tensor_copy(out=dst, in_=src)
+
+        def w_copy(s):
+            wg = work.tile([P, 4 * CH], BF16, name="wg", tag="wg", align_bytes=64, bufs=6)
+            live[("wg", s)] = wg
+            nc.scalar.copy(
+                out=wg[:].bitcast(F32).rearrange("q (c u) -> q c u", u=2),
+                in_=live[("wt", s)][:].rearrange("q (u c) -> q c u", u=2),
+            )
 
         def quantise(kind, s, width):
             p, g = s // PASSES, s % PASSES
@@ -204,37 +271,13 @@ def tile_decoder_pb_kernel(tc, h7_pre, g7, be7, W8, b8, out):
             )
 
         def sigmoid_store(p):
-            o = work.tile([P, 2 * CH], F32, name="o", tag="o")
+            o = work.tile([P, 2 * CH], F32, name="o", tag="o", bufs=NBLK)
             nc.scalar.activation(out=o[:], in_=live[("y", p)][:], func=ACT.Sigmoid)
             nc.sync.dma_start(out=out_v[:, :, p, :], in_=o[:].rearrange("n (t c) -> n t c", t=2))
 
         last = NBLK - 1
 
-        def h_transposes(s):
-            hb = psum.tile([P, 512], F32, name="hb", tag="hb", bufs=H_BANKS)
-            live[("hb", s)] = hb
-            transposes(hb, hx[s // PASSES], s % PASSES)
-
-        def w_transposes(s):
-            wt = psum.tile([P, 512], F32, name="wt", tag="wt")
-            live[("wt", s)] = wt
-            transposes(wt, wx[s // PASSES], s % PASSES)
-
-        def w_copy(s):
-            wg = work.tile([P, 4 * CH], BF16, name="wg", tag="wg", align_bytes=64)
-            live[("wg", s)] = wg
-            nc.scalar.copy(
-                out=wg[:].bitcast(F32).rearrange("q (c u) -> q c u", u=2),
-                in_=live[("wt", s)][:].rearrange("q (u c) -> q c u", u=2),
-            )
-
-        def statistics(s):
-            hab = live[("hb", s)][:].bitcast(BF16)
-            for u in range(2):
-                c = 2 * s + u
-                nc.vector.bn_stats(out=st[:, c * 6 : (c + 1) * 6], in_=hab[:, u * 512 : (u + 1) * 512])
-
-        def last_passes(s):
+        def last_pass(s):
             if s % PASSES == 0:
                 for t in range(2):
                     acc_t = psum.tile([P, 512], F32, name="acc_t", tag="hb", bufs=H_BANKS)
@@ -246,10 +289,18 @@ def tile_decoder_pb_kernel(tc, h7_pre, g7, be7, W8, b8, out):
             return range(UNIT * j, UNIT * j + UNIT) if 0 <= j < PAIRS else range(0)
 
         sig_ready = []
-        for s in passes_of(0):
-            h_transposes(s)
-        for tau in range(PAIRS + 3):
-            w_now, h_next = passes_of(tau - LAG_W), passes_of(tau + 1)
+
+        def sigmoids(n):
+            for p in sig_ready[:n]:
+                sigmoid_store(p)
+            return sig_ready[n:]
+
+        h_transposes(0)
+        gains_and_shifts()
+        h_transposes(1)
+        for tau in range(min(LAG_W, 0), PAIRS + 2):
+            now, before, older = passes_of(tau), passes_of(tau - 1), passes_of(tau - 2)
+            w_now, w_q, h_next = passes_of(tau - LAG_W), passes_of(tau - LAG_W - 1), passes_of(tau + 1) if tau >= 0 else range(0)
             for i in range(UNIT):
                 if w_now:
                     w_transposes(w_now[i])
@@ -258,52 +309,57 @@ def tile_decoder_pb_kernel(tc, h7_pre, g7, be7, W8, b8, out):
             p_mx = (tau - 4) // 2 if tau % 2 == 0 and 4 <= tau else -1
             if 0 <= p_mx < last:
                 product(p_mx)
-            for s in passes_of(tau - 2):
-                if regroup_on_gpsimd(s):
-                    regroup(s)
-            for s in passes_of(tau):
+            if older and regroup_engine(older[1]) == "gpsimd":
+                regroup(older[1])
+            for s in now:
                 statistics(s)
             p_add = (tau - 5) // 2 if tau % 2 == 1 and 5 <= tau else -1
             if 0 <= p_add < last:
                 add_bias(p_add)
-            n_now = passes_of(tau - 1)
-            if n_now:
-                norm(n_now[0], (0, 1))
-            if w_now:
-                w_copy(w_now[0])
-            if n_now:
-                norm(n_now[1], (0,))
-            if tau < PAIRS:
-                rstd_on_scalar(tau)
-                scale_and_shift(tau)
-            if n_now:
-                norm(n_now[1], (1,))
-            if w_now:
-                w_copy(w_now[1])
-            if tau >= PAIRS:
-                for p in sig_ready[:3]:
-                    sigmoid_store(p)
-                sig_ready = sig_ready[3:]
-            if 0 <= p_add < last:
                 sig_ready.append(p_add)
-            own = [s for s in passes_of(tau - 2) if not regroup_on_gpsimd(s)]
-            other = [s for s in passes_of(tau - 2) if regroup_on_gpsimd(s)]
-            w_q = passes_of(tau - LAG_W - 1)
-            for s in own:
-                regroup(s)
-            if w_q:
-                quantise("w", w_q[0], CH)
-            for s in own:
-                quantise("a", s, ROWS)
-            if w_q:
-                quantise("w", w_q[1], CH)
-            for s in other:
-                quantise("a", s, ROWS)
-            for s in passes_of(tau - 2):
+            if before:
+                norm(before[0], 0)
+                norm(before[0], 1)
+            for s in w_now[:1]:
+                w_copy(s)
+            if before:
+                norm(before[1], 0)
+            if now:
+                rstd(tau)
+            for s in w_now[1:]:
+                w_copy(s)
+            if before and regroup_engine(before[0]) == "shared":
+                regroup_part(before[0], True)
+            if before:
+                norm(before[1], 1)
+            if tau == PAIRS - 1:
+                sig_ready = sigmoids(0)
+            if tau >= PAIRS:
+                sig_ready = sigmoids(NBLK)
+            for s in w_q[:1]:
+                quantise("w", s, CH)
+            if now:
+                scale_and_shift(tau, 0)
+            if before and regroup_engine(before[0]) == "vector":
+                regroup(before[0])
+            if before and regroup_engine(before[0]) == "shared":
+                regroup_part(before[0], False)
+            if now:
+                scale_and_shift(tau, 1)
+            for s in w_q[1:]:
+                quantise("w", s, CH)
+            if older and regroup_engine(older[1]) == "vector":
+                regroup(older[1])
+            if now:
+                scale_and_shift(tau, 2)
+            if before:
+                quantise("a", before[0], ROWS)
+            if older:
+                quantise("a", older[1], ROWS)
+            for s in [*older[1:], *before[:1]]:
                 if s // PASSES == last:
-                    last_passes(s)
-        for p in sig_ready:
-            sigmoid_store(p)
+                    last_pass(s)
+        sig_ready = sigmoids(NBLK)
         for t in range(2):
             y_t = work.tile([P, CH], F32, name="y_t", tag="y_t", bufs=2)
             nc.vector.tensor_tensor(

@@ -24,7 +24,7 @@ PAIRS = STEPS // UNIT
 W_COLS = 4 * UNIT
 V_BLOCKS = ROWS // 4 - 12
 LAG_W = 0
-H_BANKS = 6
+H_BANKS = 5
 
 
 def regroup_engine(s):
@@ -94,7 +94,7 @@ def tile_decoder_pb_kernel(tc, h7_pre, g7, be7, W8, b8, out):
         live = {}
 
         def gains_and_shifts():
-            gb_t = psum.tile([P, 512], F32, name="gb_t", tag="wt")
+            gb_t = psum.tile([P, 512], F32, name="gb_t", tag="wt", bufs=2)
             gb_words = gb_raw[:].bitcast(F32)
             for u in range(2):
                 nc.tensor.transpose(gb_t[:, u * P : (u + 1) * P], gb_words[:, u : KP // 2 : 2], ident[:])
@@ -125,7 +125,7 @@ def tile_decoder_pb_kernel(tc, h7_pre, g7, be7, W8, b8, out):
             transposes(hb, "h", s)
 
         def w_transposes(s):
-            wt = psum.tile([P, 512], F32, name="wt", tag="wt")
+            wt = psum.tile([P, 512], F32, name="wt", tag="wt", bufs=2)
             live[("wt", s)] = wt
             transposes(wt, "w", s)
 

@@ -22,7 +22,8 @@ FLOPS = 2 * NBLK * ROWS * CH * K
 UNIT = 2
 PAIRS = STEPS // UNIT
 W_COLS = 4 * UNIT
-V_BLOCKS = ROWS // 4 - 12
+BLOCKS = ROWS // 4
+S_BLOCKS, G_BLOCKS = 30, 12
 LAG_W = 0
 H_BANKS = 5
 
@@ -30,7 +31,7 @@ H_BANKS = 5
 def regroup_engine(s):
     if s % 2 == 1 and s < STEPS - UNIT:
         return "gpsimd"
-    if 4 <= s < 28:
+    if s % 2 == 0 and 4 <= s < 30:
         return "shared"
     return "vector"
 
@@ -52,13 +53,15 @@ def tile_decoder_pb_kernel(tc, h7_pre, g7, be7, W8, b8, out):
 
         where = {}
 
-        def load(kind, src, p, g0, g1):
+        def load(kind, src, p, g0, g1, by_half=False):
             width = (g1 - g0) * KP
             raw = resident.tile([P, 2 * width], BF16, name="raw", tag=kind + str(p) + "_" + str(g0))
-            nc.sync.dma_start(
-                out=raw[:].rearrange("n (t k) -> n t k", t=2),
-                in_=src[p].rearrange("(t n) k -> n t k", t=2)[:, :, g0 * KP : g1 * KP],
-            )
+            halves = [slice(0, 1), slice(1, 2)] if by_half else [slice(0, 2)]
+            for t in halves:
+                nc.sync.dma_start(
+                    out=raw[:].rearrange("n (t k) -> n t k", t=2)[:, t],
+                    in_=src[p].rearrange("(t n) k -> n t k", t=2)[:, t, g0 * KP : g1 * KP],
+                )
             for g in range(g0, g1):
                 where[(kind, p * PASSES + g)] = (raw, (g - g0) * KP, width)
 
@@ -66,7 +69,7 @@ def tile_decoder_pb_kernel(tc, h7_pre, g7, be7, W8, b8, out):
         nc.vector.memset(gb_raw[64:128, :], 0.0)
         bb = const.tile([P, NBLK * CH], BF16)
 
-        load("h", h7_pre, 0, 0, 1)
+        load("h", h7_pre, 0, 0, 1, by_half=True)
         nc.scalar.dma_start(out=gb_raw[0:32, :], in_=g7.rearrange("p (g k) -> (p g) k", k=KP))
         nc.scalar.dma_start(out=gb_raw[32:64, :], in_=be7.rearrange("p (g k) -> (p g) k", k=KP))
         load("h", h7_pre, 0, 1, 2)
@@ -93,21 +96,12 @@ def tile_decoder_pb_kernel(tc, h7_pre, g7, be7, W8, b8, out):
         out_v = out.rearrange("(t n) p c -> n t p c", t=2)
         live = {}
 
-        def gains_and_shifts():
+        def gb_transposes():
             gb_t = psum.tile([P, 512], F32, name="gb_t", tag="wt", bufs=2)
             gb_words = gb_raw[:].bitcast(F32)
             for u in range(2):
                 nc.tensor.transpose(gb_t[:, u * P : (u + 1) * P], gb_words[:, u : KP // 2 : 2], ident[:])
-            gb_rows = gb_t[:, 0 : 2 * P].bitcast(BF16).rearrange("q (u r e) -> q u r e", u=2, e=2)
-            rows = NBLK * PASSES
-            for i in range(UNIT):
-                nc.vector.tensor_copy(
-                    out=gain[:].rearrange("q (j m i u e) -> q m i u j e", m=2, i=2, u=2, e=2)[:, 0, i],
-                    in_=gb_rows[:, :, i:rows:UNIT, :],
-                )
-            nc.vector.tensor_copy(
-                out=shift[:].rearrange("q (r u e) -> q u r e", u=2, e=2), in_=gb_rows[:, :, rows : 2 * rows, :]
-            )
+            return gb_t
 
         def transposes(bank, kind, s):
             raw, first, width = where[(kind, s)]
@@ -131,6 +125,18 @@ def tile_decoder_pb_kernel(tc, h7_pre, g7, be7, W8, b8, out):
 
         def unit_stats(j):
             return st[:, j * 3 * W_COLS : (j + 1) * 3 * W_COLS].rearrange("q (c s) -> q c s", s=3)
+
+        def gains_and_shifts_out(gb_t):
+            gb_rows = gb_t[:, 0 : 2 * P].bitcast(BF16).rearrange("q (u r e) -> q u r e", u=2, e=2)
+            rows = NBLK * PASSES
+            for i in range(UNIT):
+                nc.vector.tensor_copy(
+                    out=gain[:].rearrange("q (j m i u e) -> q m i u j e", m=2, i=2, u=2, e=2)[:, 0, i],
+                    in_=gb_rows[:, :, i:rows:UNIT, :],
+                )
+            nc.vector.tensor_copy(
+                out=shift[:].rearrange("q (r u e) -> q u r e", u=2, e=2), in_=gb_rows[:, :, rows : 2 * rows, :]
+            )
 
         def statistics(s):
             hab = live[("hb", s)][:].bitcast(BF16)
@@ -187,14 +193,27 @@ def tile_decoder_pb_kernel(tc, h7_pre, g7, be7, W8, b8, out):
                 else:
                     nc.scalar.activation(out=dst, in_=bank[:, u, :, e], func=ACT.Relu, bias=bias, scale=scale)
 
-        def regroup_part(s, on_scalar):
+        def shares(s):
+            g = G_BLOCKS if s < 28 else 0
+            sc_n = S_BLOCKS
+            v_end = BLOCKS - sc_n - g
+            return {"vector": (0, v_end), "scalar": (v_end, v_end + sc_n), "gpsimd": (v_end + sc_n, BLOCKS)}
+
+        def regroup_part(s, engine):
             if ("grouped", s) not in live:
                 grouped = work.tile([P, 4 * ROWS], BF16, name="grouped", tag="grouped", align_bytes=64)
                 live[("grouped", s)] = grouped
-            cols = slice(V_BLOCKS, ROWS // 4) if on_scalar else slice(0, V_BLOCKS)
-            dst = live[("grouped", s)][:].rearrange("q (c i j) -> q c j i", i=4, j=4)[:, cols]
-            src = live[("planes", s)][:].rearrange("q (j c i) -> q c j i", i=4, j=4)[:, cols]
-            if on_scalar:
+            first, end = shares(s)[engine]
+            if first == end:
+                return
+            if engine == "gpsimd":
+                dst = live[("grouped", s)][:].rearrange("q (n j) -> q n j", j=4)[:, 4 * first : 4 * end]
+                src = live[("planes", s)][:].rearrange("q (j n) -> q n j", j=4)[:, 4 * first : 4 * end]
+                nc.gpsimd.tensor_scalar(out=dst, in0=src, scalar1=1.0, scalar2=0.0, op0=ALU.mult, op1=ALU.add)
+                return
+            dst = live[("grouped", s)][:].rearrange("q (c i j) -> q c j i", i=4, j=4)[:, first:end]
+            src = live[("planes", s)][:].rearrange("q (j c i) -> q c j i", i=4, j=4)[:, first:end]
+            if engine == "scalar":
                 nc.scalar.copy(out=dst, in_=src)
             else:
                 nc.vector.tensor_copy(out=dst, in_=src)
@@ -209,6 +228,8 @@ def tile_decoder_pb_kernel(tc, h7_pre, g7, be7, W8, b8, out):
             dst = grouped[:].rearrange("q (c i j) -> q c j i", i=4, j=4)
             src = live[("planes", s)][:].rearrange("q (j c i) -> q c j i", i=4, j=4)
             if engine == "gpsimd":
+                dst = grouped[:].rearrange("q (n j) -> q n j", j=4)
+                src = live[("planes", s)][:].rearrange("q (j n) -> q n j", j=4)
                 nc.gpsimd.tensor_scalar(out=dst, in0=src, scalar1=1.0, scalar2=0.0, op0=ALU.mult, op1=ALU.add)
             elif engine == "scalar":
                 nc.scalar.copy(out=dst, in_=src)
@@ -218,25 +239,31 @@ def tile_decoder_pb_kernel(tc, h7_pre, g7, be7, W8, b8, out):
                 nc.vector.tensor_copy(out=dst, in_=src)
 
         def w_copy(s):
-            wg = work.tile([P, 4 * CH], BF16, name="wg", tag="wg", align_bytes=64, bufs=6)
-            live[("wg", s)] = wg
+            j, i = s // UNIT, s % UNIT
+            if i == 0:
+                wg = work.tile([P, UNIT * 4 * CH], BF16, name="wg", tag="wg", align_bytes=64, bufs=3)
+                live[("wg", j)] = wg
             nc.scalar.copy(
-                out=wg[:].bitcast(F32).rearrange("q (c u) -> q c u", u=2),
+                out=live[("wg", j)][:, i * 4 * CH : (i + 1) * 4 * CH].bitcast(F32).rearrange("q (c u) -> q c u", u=2),
                 in_=live[("wt", s)][:].rearrange("q (u c) -> q c u", u=2),
             )
 
-        def quantise(kind, s, width):
+        def quantise(kind, s, n, raw):
             p, g = s // PASSES, s % PASSES
+            width = ROWS if kind == "a" else CH
             if (kind, p) not in live:
                 words = codes.tile([P, PASSES * width], U32, name="words", tag=kind + "_words", align_bytes=64)
                 scales = codes.tile([P, PASSES * width], U8, name="scales", tag=kind + "_scales", align_bytes=64)
                 live[(kind, p)] = (words, scales)
             words, scales = live[(kind, p)]
-            nc.vector.quantize_mx(
-                out=words[:, g * width : (g + 1) * width].bitcast(FP8X4),
-                scales=scales[:, g * width : (g + 1) * width],
-                in_=live[("grouped" if kind == "a" else "wg", s)][:],
-            )
+            cols = slice(g * width, (g + n) * width)
+            nc.vector.quantize_mx(out=words[:, cols].bitcast(FP8X4), scales=scales[:, cols], in_=raw[:])
+
+        def quantise_w(j):
+            quantise("w", UNIT * j, UNIT, live[("wg", j)])
+
+        def quantise_a(s):
+            quantise("a", s, 1, live[("grouped", s)])
 
         def mx_pass(acc_cols, p, g, t):
             a_words, a_scales = live[("a", p)]
@@ -253,15 +280,17 @@ def tile_decoder_pb_kernel(tc, h7_pre, g7, be7, W8, b8, out):
                 stop=(g == PASSES - 1),
             )
 
-        def product(p):
-            acc = psum.tile([P, 512], F32, name="acc", tag="acc")
-            live[("acc", p)] = acc
-            for t in range(2):
+        def product(p, halves):
+            if 0 in halves:
+                acc = psum.tile([P, 512], F32, name="acc", tag="acc")
+                live[("acc", p)] = acc
+            acc = live[("acc", p)]
+            for t in halves:
                 for g in range(PASSES):
                     mx_pass(acc[:, t * CH : (t + 1) * CH], p, g, t)
 
         def add_bias(p):
-            y = work.tile([P, 2 * CH], F32, name="y", tag="y", bufs=NBLK)
+            y = work.tile([P, 2 * CH], F32, name="y", tag="y", bufs=NBLK - 1)
             live[("y", p)] = y
             nc.vector.tensor_tensor(
                 out=y[:].rearrange("n (t c) -> n t c", t=2),
@@ -271,7 +300,7 @@ def tile_decoder_pb_kernel(tc, h7_pre, g7, be7, W8, b8, out):
             )
 
         def sigmoid_store(p):
-            o = work.tile([P, 2 * CH], F32, name="o", tag="o", bufs=NBLK)
+            o = work.tile([P, 2 * CH], F32, name="o", tag="o", bufs=NBLK - 1)
             nc.scalar.activation(out=o[:], in_=live[("y", p)][:], func=ACT.Sigmoid)
             nc.sync.dma_start(out=out_v[:, :, p, :], in_=o[:].rearrange("n (t c) -> n t c", t=2))
 
@@ -285,6 +314,9 @@ def tile_decoder_pb_kernel(tc, h7_pre, g7, be7, W8, b8, out):
             for t in range(2):
                 mx_pass(live[("acc_t", t)][:, 0:CH], last, s % PASSES, t)
 
+        def late(s):
+            return G_BLOCKS > 0 and regroup_engine(s) == "shared" and s < 28
+
         def passes_of(j):
             return range(UNIT * j, UNIT * j + UNIT) if 0 <= j < PAIRS else range(0)
 
@@ -296,7 +328,7 @@ def tile_decoder_pb_kernel(tc, h7_pre, g7, be7, W8, b8, out):
             return sig_ready[n:]
 
         h_transposes(0)
-        gains_and_shifts()
+        gb_t = gb_transposes()
         h_transposes(1)
         for tau in range(min(LAG_W, 0), PAIRS + 2):
             now, before, older = passes_of(tau), passes_of(tau - 1), passes_of(tau - 2)
@@ -306,17 +338,24 @@ def tile_decoder_pb_kernel(tc, h7_pre, g7, be7, W8, b8, out):
                     w_transposes(w_now[i])
                 if h_next:
                     h_transposes(h_next[i])
-            p_mx = (tau - 4) // 2 if tau % 2 == 0 and 4 <= tau else -1
-            if 0 <= p_mx < last:
-                product(p_mx)
+            p_mx = (tau - 4) // 2 if 4 <= tau else -1
+            if 0 <= p_mx < last - 1:
+                if p_mx < NBLK - 3:
+                    product(p_mx, (tau % 2,))
+                elif tau % 2 == 0:
+                    product(p_mx, (0, 1))
             if older and regroup_engine(older[1]) == "gpsimd":
                 regroup(older[1])
-            for s in now:
-                statistics(s)
-            p_add = (tau - 5) // 2 if tau % 2 == 1 and 5 <= tau else -1
+            if older and late(older[0]):
+                regroup_part(older[0], "gpsimd")
+            p_add = (tau - 6) // 2 if tau % 2 == 0 and 6 <= tau < PAIRS else (tau - 5) // 2 if tau == PAIRS - 1 else -1
             if 0 <= p_add < last:
                 add_bias(p_add)
                 sig_ready.append(p_add)
+            for s in now:
+                statistics(s)
+                if s == 0:
+                    gains_and_shifts_out(gb_t)
             if before:
                 norm(before[0], 0)
                 norm(before[0], 1)
@@ -324,38 +363,53 @@ def tile_decoder_pb_kernel(tc, h7_pre, g7, be7, W8, b8, out):
                 w_copy(s)
             if before:
                 norm(before[1], 0)
+            if before and regroup_engine(before[0]) == "shared":
+                regroup_part(before[0], "scalar")
             if now:
                 rstd(tau)
             for s in w_now[1:]:
                 w_copy(s)
-            if before and regroup_engine(before[0]) == "shared":
-                regroup_part(before[0], True)
             if before:
                 norm(before[1], 1)
             if tau == PAIRS - 1:
                 sig_ready = sigmoids(0)
-            if tau >= PAIRS:
+            if tau == PAIRS:
+                add_bias(last - 1)
                 sig_ready = sigmoids(NBLK)
-            for s in w_q[:1]:
-                quantise("w", s, CH)
-            if now:
+                sigmoid_store(last - 1)
+            ending = tau >= PAIRS - 1
+            if w_q and not ending:
+                quantise_w(tau - LAG_W - 1)
+            if now and not ending:
                 scale_and_shift(tau, 0)
-            if before and regroup_engine(before[0]) == "vector":
+            if before and regroup_engine(before[0]) == "vector" and not ending:
                 regroup(before[0])
             if before and regroup_engine(before[0]) == "shared":
-                regroup_part(before[0], False)
-            if now:
-                scale_and_shift(tau, 1)
-            for s in w_q[1:]:
-                quantise("w", s, CH)
+                regroup_part(before[0], "vector")
+            if now and ending:
+                scale_and_shift(tau, 0)
             if older and regroup_engine(older[1]) == "vector":
                 regroup(older[1])
             if now:
+                scale_and_shift(tau, 1)
+            if w_q and ending:
+                quantise_w(tau - LAG_W - 1)
+            if now and ending:
                 scale_and_shift(tau, 2)
-            if before:
-                quantise("a", before[0], ROWS)
+            if before and regroup_engine(before[0]) == "vector" and ending:
+                regroup(before[0])
+            if older and late(older[0]):
+                quantise_a(older[0])
+            if before and not late(before[0]) and not ending:
+                quantise_a(before[0])
+            if now and not ending:
+                scale_and_shift(tau, 2)
             if older:
-                quantise("a", older[1], ROWS)
+                quantise_a(older[1])
+                if older[1] == last * PASSES - 1:
+                    product(last - 1, (0, 1))
+            if before and ending:
+                quantise_a(before[0])
             for s in [*older[1:], *before[:1]]:
                 if s // PASSES == last:
                     last_pass(s)

@@ -23,7 +23,8 @@ UNIT = 2
 PAIRS = STEPS // UNIT
 W_COLS = 4 * UNIT
 BLOCKS = ROWS // 4
-S_BLOCKS, G_BLOCKS = 30, 12
+S_BLOCKS, G_BLOCKS = 22, 24
+FINE_BLOCKS = 3
 LAG_W = 0
 H_BANKS = 5
 
@@ -70,16 +71,18 @@ def tile_decoder_pb_kernel(tc, h7_pre, g7, be7, W8, b8, out):
         bb = const.tile([P, NBLK * CH], BF16)
 
         load("h", h7_pre, 0, 0, 1, by_half=True)
-        nc.scalar.dma_start(out=gb_raw[0:32, :], in_=g7.rearrange("p (g k) -> (p g) k", k=KP))
-        nc.scalar.dma_start(out=gb_raw[32:64, :], in_=be7.rearrange("p (g k) -> (p g) k", k=KP))
         load("h", h7_pre, 0, 1, 2)
-        load("w", W8, 0, 0, 2)
-        load("h", h7_pre, 0, 2, 4)
+        nc.sync.dma_start(out=gb_raw[0:32, :], in_=g7.rearrange("p (g k) -> (p g) k", k=KP))
+        nc.sync.dma_start(out=gb_raw[32:64, :], in_=be7.rearrange("p (g k) -> (p g) k", k=KP))
+        for g in range(2):
+            load("w", W8, 0, g, g + 1)
+            load("h", h7_pre, 0, g + 2, g + 3)
         load("w", W8, 0, 2, 4)
         for p in range(1, NBLK):
-            load("h", h7_pre, p, 0, PASSES)
-            load("w", W8, p, 0, PASSES)
-            if p == 1:
+            for g0, g1 in [(0, UNIT), (UNIT, PASSES)] if p < FINE_BLOCKS else [(0, PASSES)]:
+                load("h", h7_pre, p, g0, g1)
+                load("w", W8, p, g0, g1)
+            if p == 3:
                 nc.sync.dma_start(out=bb[:], in_=b8.rearrange("p c -> (p c)").partition_broadcast(P))
 
         ident = const.tile([P, P], F32)
@@ -130,11 +133,11 @@ def tile_decoder_pb_kernel(tc, h7_pre, g7, be7, W8, b8, out):
             gb_rows = gb_t[:, 0 : 2 * P].bitcast(BF16).rearrange("q (u r e) -> q u r e", u=2, e=2)
             rows = NBLK * PASSES
             for i in range(UNIT):
-                nc.vector.tensor_copy(
+                nc.scalar.copy(
                     out=gain[:].rearrange("q (j m i u e) -> q m i u j e", m=2, i=2, u=2, e=2)[:, 0, i],
                     in_=gb_rows[:, :, i:rows:UNIT, :],
                 )
-            nc.vector.tensor_copy(
+            nc.scalar.copy(
                 out=shift[:].rearrange("q (r u e) -> q u r e", u=2, e=2), in_=gb_rows[:, :, rows : 2 * rows, :]
             )
 
@@ -327,9 +330,9 @@ def tile_decoder_pb_kernel(tc, h7_pre, g7, be7, W8, b8, out):
                 sigmoid_store(p)
             return sig_ready[n:]
 
-        h_transposes(0)
+        for s in passes_of(0):
+            h_transposes(s)
         gb_t = gb_transposes()
-        h_transposes(1)
         for tau in range(min(LAG_W, 0), PAIRS + 2):
             now, before, older = passes_of(tau), passes_of(tau - 1), passes_of(tau - 2)
             w_now, w_q, h_next = passes_of(tau - LAG_W), passes_of(tau - LAG_W - 1), passes_of(tau + 1) if tau >= 0 else range(0)
@@ -354,10 +357,12 @@ def tile_decoder_pb_kernel(tc, h7_pre, g7, be7, W8, b8, out):
                 sig_ready.append(p_add)
             for s in now:
                 statistics(s)
-                if s == 0:
-                    gains_and_shifts_out(gb_t)
+            if tau == 0:
+                gains_and_shifts_out(gb_t)
             if before:
                 norm(before[0], 0)
+                if tau == 1:
+                    w_copy(1)
                 norm(before[0], 1)
             for s in w_now[:1]:
                 w_copy(s)
@@ -367,8 +372,9 @@ def tile_decoder_pb_kernel(tc, h7_pre, g7, be7, W8, b8, out):
                 regroup_part(before[0], "scalar")
             if now:
                 rstd(tau)
-            for s in w_now[1:]:
-                w_copy(s)
+            if tau > 0:
+                for s in w_now[1:]:
+                    w_copy(s)
             if before:
                 norm(before[1], 1)
             if tau == PAIRS - 1:

@@ -23,8 +23,9 @@ UNIT = 2
 PAIRS = STEPS // UNIT
 W_COLS = 4 * UNIT
 BLOCKS = ROWS // 4
-S_BLOCKS, G_BLOCKS = 22, 24
+S_BLOCKS, G_BLOCKS = (20, 26), (24, 8)
 FINE_BLOCKS = 3
+EARLY_SIGMOIDS = 3
 LAG_W = 0
 H_BANKS = 5
 
@@ -196,9 +197,17 @@ def tile_decoder_pb_kernel(tc, h7_pre, g7, be7, W8, b8, out):
                 else:
                     nc.scalar.activation(out=dst, in_=bank[:, u, :, e], func=ACT.Relu, bias=bias, scale=scale)
 
+        def bias_block(tau):
+            if tau == PAIRS - 1:
+                return NBLK - 3
+            return (tau - 6) // 2 if tau % 2 == 0 and 6 <= tau < PAIRS else -1
+
+        def share_kind(s):
+            return 0 if bias_block(s // UNIT + 2) >= 0 else 1
+
         def shares(s):
-            g = G_BLOCKS if s < 28 else 0
-            sc_n = S_BLOCKS
+            g = G_BLOCKS[share_kind(s)] if s < 28 else 0
+            sc_n = S_BLOCKS[share_kind(s)]
             v_end = BLOCKS - sc_n - g
             return {"vector": (0, v_end), "scalar": (v_end, v_end + sc_n), "gpsimd": (v_end + sc_n, BLOCKS)}
 
@@ -268,7 +277,7 @@ def tile_decoder_pb_kernel(tc, h7_pre, g7, be7, W8, b8, out):
         def quantise_a(s):
             quantise("a", s, 1, live[("grouped", s)])
 
-        def mx_pass(acc_cols, p, g, t):
+        def mx_pass(acc_cols, p, g, t, g_last=PASSES - 1):
             a_words, a_scales = live[("a", p)]
             w_words, w_scales = live[("w", p)]
             a_cols = slice(g * ROWS + t * P, g * ROWS + (t + 1) * P)
@@ -280,7 +289,7 @@ def tile_decoder_pb_kernel(tc, h7_pre, g7, be7, W8, b8, out):
                 rhs=w_words[:, w_cols].bitcast(FP8X4),
                 rhs_scale=w_scales[:, w_cols],
                 start=(g == 0),
-                stop=(g == PASSES - 1),
+                stop=(g == g_last),
             )
 
         def product(p, halves):
@@ -315,10 +324,10 @@ def tile_decoder_pb_kernel(tc, h7_pre, g7, be7, W8, b8, out):
                     acc_t = psum.tile([P, 512], F32, name="acc_t", tag="hb", bufs=H_BANKS)
                     live[("acc_t", t)] = acc_t
             for t in range(2):
-                mx_pass(live[("acc_t", t)][:, 0:CH], last, s % PASSES, t)
+                mx_pass(live[("acc_t", t)][:, 0:CH], last, s % PASSES, t, PASSES - 2)
 
         def late(s):
-            return G_BLOCKS > 0 and regroup_engine(s) == "shared" and s < 28
+            return regroup_engine(s) == "shared" and s < 28
 
         def passes_of(j):
             return range(UNIT * j, UNIT * j + UNIT) if 0 <= j < PAIRS else range(0)
@@ -333,7 +342,7 @@ def tile_decoder_pb_kernel(tc, h7_pre, g7, be7, W8, b8, out):
         for s in passes_of(0):
             h_transposes(s)
         gb_t = gb_transposes()
-        for tau in range(min(LAG_W, 0), PAIRS + 2):
+        for tau in range(min(LAG_W, 0), PAIRS + 1):
             now, before, older = passes_of(tau), passes_of(tau - 1), passes_of(tau - 2)
             w_now, w_q, h_next = passes_of(tau - LAG_W), passes_of(tau - LAG_W - 1), passes_of(tau + 1) if tau >= 0 else range(0)
             for i in range(UNIT):
@@ -351,32 +360,39 @@ def tile_decoder_pb_kernel(tc, h7_pre, g7, be7, W8, b8, out):
                 regroup(older[1])
             if older and late(older[0]):
                 regroup_part(older[0], "gpsimd")
-            p_add = (tau - 6) // 2 if tau % 2 == 0 and 6 <= tau < PAIRS else (tau - 5) // 2 if tau == PAIRS - 1 else -1
-            if 0 <= p_add < last:
+            p_add = bias_block(tau)
+            if p_add >= 0:
                 add_bias(p_add)
                 sig_ready.append(p_add)
             for s in now:
                 statistics(s)
+            if tau == PAIRS:
+                sig_ready = sigmoids(EARLY_SIGMOIDS)
             if tau == 0:
                 gains_and_shifts_out(gb_t)
+                rstd(0)
             if before:
                 norm(before[0], 0)
                 if tau == 1:
                     w_copy(1)
                 norm(before[0], 1)
-            for s in w_now[:1]:
+            for s in w_now[:1] if tau != 1 else []:
                 w_copy(s)
             if before:
                 norm(before[1], 0)
             if before and regroup_engine(before[0]) == "shared":
                 regroup_part(before[0], "scalar")
-            if now:
+            if now and tau > 0:
                 rstd(tau)
-            if tau > 0:
+            if tau == 1:
+                w_copy(2)
+            if tau > 1:
                 for s in w_now[1:]:
                     w_copy(s)
             if before:
                 norm(before[1], 1)
+            if tau == 1:
+                w_copy(3)
             if tau == PAIRS - 1:
                 sig_ready = sigmoids(0)
             if tau == PAIRS:
@@ -394,12 +410,20 @@ def tile_decoder_pb_kernel(tc, h7_pre, g7, be7, W8, b8, out):
                 regroup_part(before[0], "vector")
             if now and ending:
                 scale_and_shift(tau, 0)
-            if older and regroup_engine(older[1]) == "vector":
+            if older and regroup_engine(older[1]) == "vector" and not ending:
                 regroup(older[1])
             if now:
                 scale_and_shift(tau, 1)
             if w_q and ending:
                 quantise_w(tau - LAG_W - 1)
+            if tau == PAIRS:
+                quantise_a(older[1])
+                last_pass(older[1])
+                for s in reversed(before):
+                    regroup(s)
+                    quantise_a(s)
+                    last_pass(s)
+                break
             if now and ending:
                 scale_and_shift(tau, 2)
             if before and regroup_engine(before[0]) == "vector" and ending:

from contextlib import ExitStack

import concourse.mybir as mybir
from concourse.masks import make_identity

F32 = mybir.dt.float32
BF16 = mybir.dt.bfloat16
U32 = mybir.dt.uint32
U8 = mybir.dt.uint8
FP8X4 = mybir.dt.float8_e4m3fn_x4
ALU = mybir.AluOpType
ACT = mybir.ActivationFunctionType

NBLK, ROWS, K, CH = 8, 256, 2048, 256
EPS = 1e-5
P = 128
KP = 512
PASSES = K // KP
STEPS = NBLK * PASSES
FLOPS = 2 * NBLK * ROWS * CH * K

UNIT = 2
PAIRS = STEPS // UNIT
W_COLS = 4 * UNIT
BLOCKS = ROWS // 4
S_BLOCKS, G_BLOCKS = (20, 26), (24, 8)
FINE_BLOCKS = 3
EARLY_SIGMOIDS = 3
LAG_W = 0
H_BANKS = 5


def regroup_engine(s):
    if s % 2 == 1 and s < STEPS - UNIT:
        return "gpsimd"
    if s % 2 == 0 and 4 <= s < 30:
        return "shared"
    return "vector"


def norm_on_vector(s):
    return s == STEPS - 1


def tile_decoder_pb_kernel(tc, h7_pre, g7, be7, W8, b8, out):
    nc = tc.nc
    with ExitStack() as ctx:
        const = ctx.enter_context(tc.tile_pool(name="const", bufs=1))
        resident = ctx.enter_context(tc.tile_pool(name="resident", bufs=1))
        small = ctx.enter_context(tc.tile_pool(name="small", bufs=4))
        work = ctx.enter_context(tc.tile_pool(name="work", bufs=4))
        codes = ctx.enter_context(tc.tile_pool(name="codes", bufs=3))
        psum = ctx.enter_context(tc.psum_pool(name="psum", bufs=1))
        ctx.enter_context(tc.manual_schedule())

        where = {}

        def load(kind, src, p, g0, g1, by_half=False):
            width = (g1 - g0) * KP
            raw = resident.tile([P, 2 * width], BF16, name="raw", tag=kind + str(p) + "_" + str(g0))
            halves = [slice(0, 1), slice(1, 2)] if by_half else [slice(0, 2)]
            for t in halves:
                nc.sync.dma_start(
                    out=raw[:].rearrange("n (t k) -> n t k", t=2)[:, t],
                    in_=src[p].rearrange("(t n) k -> n t k", t=2)[:, t, g0 * KP : g1 * KP],
                )
            for g in range(g0, g1):
                where[(kind, p * PASSES + g)] = (raw, (g - g0) * KP, width)

        gb_raw = const.tile([P, KP], BF16)
        nc.vector.memset(gb_raw[64:128, :], 0.0)
        bb = const.tile([P, NBLK * CH], BF16)

        load("h", h7_pre, 0, 0, 1, by_half=True)
        load("h", h7_pre, 0, 1, 2)
        nc.sync.dma_start(out=gb_raw[0:32, :], in_=g7.rearrange("p (g k) -> (p g) k", k=KP))
        nc.sync.dma_start(out=gb_raw[32:64, :], in_=be7.rearrange("p (g k) -> (p g) k", k=KP))
        for g in range(2):
            load("w", W8, 0, g, g + 1)
            load("h", h7_pre, 0, g + 2, g + 3)
        load("w", W8, 0, 2, 4)
        for p in range(1, NBLK):
            for g0, g1 in [(0, UNIT), (UNIT, PASSES)] if p < FINE_BLOCKS else [(0, PASSES)]:
                load("h", h7_pre, p, g0, g1)
                load("w", W8, p, g0, g1)
            if p == 3:
                nc.sync.dma_start(out=bb[:], in_=b8.rearrange("p c -> (p c)").partition_broadcast(P))

        ident = const.tile([P, P], F32)
        make_identity(nc, ident[:])
        warm = const.tile([P, 1], F32)
        nc.vector.memset(warm[:], 1.0)
        nc.scalar.activation(out=warm[:], in_=warm[:], func=ACT.Abs_reciprocal_sqrt)

        st = const.tile([P, NBLK * 16 * 3], F32)
        gain = const.tile([P, NBLK * 32], F32)
        shift = const.tile([P, NBLK * 16], F32)
        sc = const.tile([P, NBLK * 32], F32)
        bi = const.tile([P, NBLK * 16], F32)
        out_v = out.rearrange("(t n) p c -> n t p c", t=2)
        live = {}

        def gb_transposes():
            gb_t = psum.tile([P, 512], F32, name="gb_t", tag="wt", bufs=2)
            gb_words = gb_raw[:].bitcast(F32)
            for u in range(2):
                nc.tensor.transpose(gb_t[:, u * P : (u + 1) * P], gb_words[:, u : KP // 2 : 2], ident[:])
            return gb_t

        def transposes(bank, kind, s):
            raw, first, width = where[(kind, s)]
            words = raw[:].bitcast(F32)
            for u in range(2):
                for t in range(2):
                    w0 = (t * width + first) // 2 + u
                    nc.tensor.transpose(
                        bank[:, u * 256 + t * P : u * 256 + (t + 1) * P], words[:, w0 : w0 - u + 256 : 2], ident[:]
                    )

        def h_transposes(s):
            hb = psum.tile([P, 512], F32, name="hb", tag="hb", bufs=H_BANKS)
            live[("hb", s)] = hb
            transposes(hb, "h", s)

        def w_transposes(s):
            wt = psum.tile([P, 512], F32, name="wt", tag="wt", bufs=2)
            live[("wt", s)] = wt
            transposes(wt, "w", s)

        def unit_stats(j):
            return st[:, j * 3 * W_COLS : (j + 1) * 3 * W_COLS].rearrange("q (c s) -> q c s", s=3)

        def gains_and_shifts_out(gb_t):
            gb_rows = gb_t[:, 0 : 2 * P].bitcast(BF16).rearrange("q (u r e) -> q u r e", u=2, e=2)
            rows = NBLK * PASSES
            for i in range(UNIT):
                nc.scalar.copy(
                    out=gain[:].rearrange("q (j m i u e) -> q m i u j e", m=2, i=2, u=2, e=2)[:, 0, i],
                    in_=gb_rows[:, :, i:rows:UNIT, :],
                )
            nc.scalar.copy(
                out=shift[:].rearrange("q (r u e) -> q u r e", u=2, e=2), in_=gb_rows[:, :, rows : 2 * rows, :]
            )

        def statistics(s):
            hab = live[("hb", s)][:].bitcast(BF16)
            for u in range(2):
                c = 2 * s + u
                nc.vector.bn_stats(out=st[:, c * 6 : (c + 1) * 6], in_=hab[:, u * 512 : (u + 1) * 512])

        def rstd(j):
            r = small.tile([P, W_COLS], F32, name="r", tag="r")
            live[("rstd", j)] = r
            nc.scalar.activation(
                out=r[:], in_=unit_stats(j)[:, :, 2], func=ACT.Abs_reciprocal_sqrt, scale=1.0 / ROWS, bias=EPS
            )

        def scale_and_shift(j, part):
            w = W_COLS
            gains, both = gain[:, 2 * j * w : (2 * j + 1) * w], slice(2 * j * w, (2 * j + 2) * w)
            if part == 0:
                nc.vector.tensor_tensor(
                    out=gain[:, (2 * j + 1) * w : (2 * j + 2) * w], in0=unit_stats(j)[:, :, 1], in1=gains, op=ALU.mult
                )
            elif part == 1:
                nc.vector.tensor_tensor(
                    out=sc[:, both].rearrange("q (m c) -> q m c", m=2),
                    in0=gain[:, both].rearrange("q (m c) -> q m c", m=2),
                    in1=live[("rstd", j)][:].unsqueeze(1).to_broadcast([P, 2, w]),
                    op=ALU.mult,
                )
            else:
                nc.vector.tensor_tensor(
                    out=bi[:, j * w : (j + 1) * w],
                    in0=shift[:, j * w : (j + 1) * w],
                    in1=sc[:, (2 * j + 1) * w : (2 * j + 2) * w],
                    op=ALU.subtract,
                )

        def norm(s, u):
            bank = live[("hb", s)][:].bitcast(BF16).rearrange("q (u n e) -> q u n e", u=2, e=2)
            if u == 0:
                planes = work.tile([P, 4 * ROWS], BF16, name="planes", tag="planes", bufs=6)
                live[("planes", s)] = planes
            planes = live[("planes", s)]
            for e in range(2):
                c = s % UNIT * 4 + u * 2 + e
                sc_col = s // UNIT * 2 * W_COLS + c
                bi_col = s // UNIT * W_COLS + c
                j = 2 * u + e
                dst = planes[:, j * ROWS : (j + 1) * ROWS]
                scale, bias = sc[:, sc_col : sc_col + 1], bi[:, bi_col : bi_col + 1]
                if norm_on_vector(s):
                    nc.vector.tensor_scalar(
                        out=dst, in0=bank[:, u, :, e], scalar1=scale, scalar2=bias, op0=ALU.mult, op1=ALU.add
                    )
                else:
                    nc.scalar.activation(out=dst, in_=bank[:, u, :, e], func=ACT.Relu, bias=bias, scale=scale)

        def bias_block(tau):
            if tau == PAIRS - 1:
                return NBLK - 3
            return (tau - 6) // 2 if tau % 2 == 0 and 6 <= tau < PAIRS else -1

        def share_kind(s):
            return 0 if bias_block(s // UNIT + 2) >= 0 else 1

        def shares(s):
            g = G_BLOCKS[share_kind(s)] if s < 28 else 0
            sc_n = S_BLOCKS[share_kind(s)]
            v_end = BLOCKS - sc_n - g
            return {"vector": (0, v_end), "scalar": (v_end, v_end + sc_n), "gpsimd": (v_end + sc_n, BLOCKS)}

        def regroup_part(s, engine):
            if ("grouped", s) not in live:
                grouped = work.tile([P, 4 * ROWS], BF16, name="grouped", tag="grouped", align_bytes=64)
                live[("grouped", s)] = grouped
            first, end = shares(s)[engine]
            if first == end:
                return
            if engine == "gpsimd":
                dst = live[("grouped", s)][:].rearrange("q (n j) -> q n j", j=4)[:, 4 * first : 4 * end]
                src = live[("planes", s)][:].rearrange("q (j n) -> q n j", j=4)[:, 4 * first : 4 * end]
                nc.gpsimd.tensor_scalar(out=dst, in0=src, scalar1=1.0, scalar2=0.0, op0=ALU.mult, op1=ALU.add)
                return
            dst = live[("grouped", s)][:].rearrange("q (c i j) -> q c j i", i=4, j=4)[:, first:end]
            src = live[("planes", s)][:].rearrange("q (j c i) -> q c j i", i=4, j=4)[:, first:end]
            if engine == "scalar":
                nc.scalar.copy(out=dst, in_=src)
            else:
                nc.vector.tensor_copy(out=dst, in_=src)

        def regroup(s):
            engine = regroup_engine(s)
            if engine == "gpsimd":
                grouped = work.tile([P, 4 * ROWS], BF16, name="grouped_g", tag="grouped_g", align_bytes=64, bufs=1)
            else:
                grouped = work.tile([P, 4 * ROWS], BF16, name="grouped", tag="grouped", align_bytes=64)
            live[("grouped", s)] = grouped
            dst = grouped[:].rearrange("q (c i j) -> q c j i", i=4, j=4)
            src = live[("planes", s)][:].rearrange("q (j c i) -> q c j i", i=4, j=4)
            if engine == "gpsimd":
                dst = grouped[:].rearrange("q (n j) -> q n j", j=4)
                src = live[("planes", s)][:].rearrange("q (j n) -> q n j", j=4)
                nc.gpsimd.tensor_scalar(out=dst, in0=src, scalar1=1.0, scalar2=0.0, op0=ALU.mult, op1=ALU.add)
            elif engine == "scalar":
                nc.scalar.copy(out=dst, in_=src)
            elif norm_on_vector(s):
                nc.vector.tensor_scalar(out=dst, in0=src, scalar1=0.0, scalar2=None, op0=ALU.max)
            else:
                nc.vector.tensor_copy(out=dst, in_=src)

        def w_copy(s):
            j, i = s // UNIT, s % UNIT
            if i == 0:
                wg = work.tile([P, UNIT * 4 * CH], BF16, name="wg", tag="wg", align_bytes=64, bufs=3)
                live[("wg", j)] = wg
            nc.scalar.copy(
                out=live[("wg", j)][:, i * 4 * CH : (i + 1) * 4 * CH].bitcast(F32).rearrange("q (c u) -> q c u", u=2),
                in_=live[("wt", s)][:].rearrange("q (u c) -> q c u", u=2),
            )

        def quantise(kind, s, n, raw):
            p, g = s // PASSES, s % PASSES
            width = ROWS if kind == "a" else CH
            if (kind, p) not in live:
                words = codes.tile([P, PASSES * width], U32, name="words", tag=kind + "_words", align_bytes=64)
                scales = codes.tile([P, PASSES * width], U8, name="scales", tag=kind + "_scales", align_bytes=64)
                live[(kind, p)] = (words, scales)
            words, scales = live[(kind, p)]
            cols = slice(g * width, (g + n) * width)
            nc.vector.quantize_mx(out=words[:, cols].bitcast(FP8X4), scales=scales[:, cols], in_=raw[:])

        def quantise_w(j):
            quantise("w", UNIT * j, UNIT, live[("wg", j)])

        def quantise_a(s):
            quantise("a", s, 1, live[("grouped", s)])

        def mx_pass(acc_cols, p, g, t, g_last=PASSES - 1):
            a_words, a_scales = live[("a", p)]
            w_words, w_scales = live[("w", p)]
            a_cols = slice(g * ROWS + t * P, g * ROWS + (t + 1) * P)
            w_cols = slice(g * CH, (g + 1) * CH)
            nc.tensor.matmul_mx(
                out=acc_cols,
                lhsT=a_words[:, a_cols].bitcast(FP8X4),
                lhsT_scale=a_scales[:, a_cols],
                rhs=w_words[:, w_cols].bitcast(FP8X4),
                rhs_scale=w_scales[:, w_cols],
                start=(g == 0),
                stop=(g == g_last),
            )

        def product(p, halves):
            if 0 in halves:
                acc = psum.tile([P, 512], F32, name="acc", tag="acc")
                live[("acc", p)] = acc
            acc = live[("acc", p)]
            for t in halves:
                for g in range(PASSES):
                    mx_pass(acc[:, t * CH : (t + 1) * CH], p, g, t)

        def add_bias(p):
            y = work.tile([P, 2 * CH], F32, name="y", tag="y", bufs=NBLK - 1)
            live[("y", p)] = y
            nc.vector.tensor_tensor(
                out=y[:].rearrange("n (t c) -> n t c", t=2),
                in0=live[("acc", p)][:].rearrange("n (t c) -> n t c", t=2),
                in1=bb[:, p * CH : (p + 1) * CH].unsqueeze(1).to_broadcast([P, 2, CH]),
                op=ALU.add,
            )

        def sigmoid_store(p):
            o = work.tile([P, 2 * CH], F32, name="o", tag="o", bufs=NBLK - 1)
            nc.scalar.activation(out=o[:], in_=live[("y", p)][:], func=ACT.Sigmoid)
            nc.sync.dma_start(out=out_v[:, :, p, :], in_=o[:].rearrange("n (t c) -> n t c", t=2))

        last = NBLK - 1

        def last_pass(s):
            if s % PASSES == 0:
                for t in range(2):
                    acc_t = psum.tile([P, 512], F32, name="acc_t", tag="hb", bufs=H_BANKS)
                    live[("acc_t", t)] = acc_t
            for t in range(2):
                mx_pass(live[("acc_t", t)][:, 0:CH], last, s % PASSES, t, PASSES - 2)

        def late(s):
            return regroup_engine(s) == "shared" and s < 28

        def passes_of(j):
            return range(UNIT * j, UNIT * j + UNIT) if 0 <= j < PAIRS else range(0)

        sig_ready = []

        def sigmoids(n):
            for p in sig_ready[:n]:
                sigmoid_store(p)
            return sig_ready[n:]

        for s in passes_of(0):
            h_transposes(s)
        gb_t = gb_transposes()
        for tau in range(min(LAG_W, 0), PAIRS + 1):
            now, before, older = passes_of(tau), passes_of(tau - 1), passes_of(tau - 2)
            w_now, w_q, h_next = passes_of(tau - LAG_W), passes_of(tau - LAG_W - 1), passes_of(tau + 1) if tau >= 0 else range(0)
            for i in range(UNIT):
                if w_now:
                    w_transposes(w_now[i])
                if h_next:
                    h_transposes(h_next[i])
            p_mx = (tau - 4) // 2 if 4 <= tau else -1
            if 0 <= p_mx < last - 1:
                if p_mx < NBLK - 3:
                    product(p_mx, (tau % 2,))
                elif tau % 2 == 0:
                    product(p_mx, (0, 1))
            if older and regroup_engine(older[1]) == "gpsimd":
                regroup(older[1])
            if older and late(older[0]):
                regroup_part(older[0], "gpsimd")
            p_add = bias_block(tau)
            if p_add >= 0:
                add_bias(p_add)
                sig_ready.append(p_add)
            for s in now:
                statistics(s)
            if tau == PAIRS:
                sig_ready = sigmoids(EARLY_SIGMOIDS)
            if tau == 0:
                gains_and_shifts_out(gb_t)
                rstd(0)
            if before:
                norm(before[0], 0)
                if tau == 1:
                    w_copy(1)
                norm(before[0], 1)
            for s in w_now[:1] if tau != 1 else []:
                w_copy(s)
            if before:
                norm(before[1], 0)
            if before and regroup_engine(before[0]) == "shared":
                regroup_part(before[0], "scalar")
            if now and tau > 0:
                rstd(tau)
            if tau == 1:
                w_copy(2)
            if tau > 1:
                for s in w_now[1:]:
                    w_copy(s)
            if before:
                norm(before[1], 1)
            if tau == 1:
                w_copy(3)
            if tau == PAIRS - 1:
                sig_ready = sigmoids(0)
            if tau == PAIRS:
                add_bias(last - 1)
                sig_ready = sigmoids(NBLK)
                sigmoid_store(last - 1)
            ending = tau >= PAIRS - 1
            if w_q and not ending:
                quantise_w(tau - LAG_W - 1)
            if now and not ending:
                scale_and_shift(tau, 0)
            if before and regroup_engine(before[0]) == "vector" and not ending:
                regroup(before[0])
            if before and regroup_engine(before[0]) == "shared":
                regroup_part(before[0], "vector")
            if now and ending:
                scale_and_shift(tau, 0)
            if older and regroup_engine(older[1]) == "vector" and not ending:
                regroup(older[1])
            if now:
                scale_and_shift(tau, 1)
            if w_q and ending:
                quantise_w(tau - LAG_W - 1)
            if tau == PAIRS:
                quantise_a(older[1])
                last_pass(older[1])
                for s in reversed(before):
                    regroup(s)
                    quantise_a(s)
                    last_pass(s)
                break
            if now and ending:
                scale_and_shift(tau, 2)
            if before and regroup_engine(before[0]) == "vector" and ending:
                regroup(before[0])
            if older and late(older[0]):
                quantise_a(older[0])
            if before and not late(before[0]) and not ending:
                quantise_a(before[0])
            if now and not ending:
                scale_and_shift(tau, 2)
            if older:
                quantise_a(older[1])
                if older[1] == last * PASSES - 1:
                    product(last - 1, (0, 1))
            if before and ending:
                quantise_a(before[0])
            for s in [*older[1:], *before[:1]]:
                if s // PASSES == last:
                    last_pass(s)
        sig_ready = sigmoids(NBLK)
        for t in range(2):
            y_t = work.tile([P, CH], F32, name="y_t", tag="y_t", bufs=2)
            nc.vector.tensor_tensor(
                out=y_t[:], in0=live[("acc_t", t)][:, 0:CH], in1=bb[:, last * CH : (last + 1) * CH], op=ALU.add
            )
            o_t = work.tile([P, CH], F32, name="o_t", tag="o_t", bufs=2)
            nc.scalar.activation(out=o_t[:], in_=y_t[:], func=ACT.Sigmoid)
            nc.sync.dma_start(out=out_v[:, t, last, :], in_=o_t[:])
